import numpy as np
import ml_dtypes


def mxq(x, axis, fmt="e4m3"):
    dtype, down = {"e4m3": (ml_dtypes.float8_e4m3fn, 7), "e5m2": (ml_dtypes.float8_e5m2, 14)}[fmt]
    v = np.moveaxis(np.asarray(x, np.float32).astype(ml_dtypes.bfloat16).astype(np.float64), axis, -1)
    blocks = v.reshape(v.shape[:-1] + (-1, 32))
    amax = np.abs(blocks).max(-1, keepdims=True)
    byte = np.maximum(np.where(amax > 0, np.frexp(amax)[1] - 1 + 127, 0) - down, 1)
    scale = np.exp2(byte - 127.0)
    codes = (blocks / scale).astype(np.float32).astype(dtype).astype(np.float64)
    return np.moveaxis((codes * scale).reshape(v.shape), -1, axis)


WIDE = False


def mx_kscale(k):
    if not WIDE:
        return np.ones(k)
    levels = np.array([10, -10, 5, -5, 0])
    a = np.random.permutation(np.resize(levels, k // 512 * 4)).reshape(k // 512, 4)
    idx = np.arange(k)
    return np.exp2(a[idx // 512, idx % 128 // 32])


BF16 = ml_dtypes.bfloat16


def bf(x):
    return np.asarray(x, np.float32).astype(BF16)


def f64(x):
    return np.asarray(x).astype(np.float64)


B, N, D, H, L = 128, 4096, 512, 8192, 512


def setup_inputs():
    s = mx_kscale(H)
    return {"h": bf(np.tanh(np.random.standard_normal((B, H)) * 0.85) * s),
            "Wm": bf(np.random.standard_normal((H, L)) * 1.2 / np.sqrt(H) / s[:, None]),
            "bm": bf(np.random.standard_normal(L) * 0.2),
            "Wv": bf(np.random.standard_normal((H, L)) * 1.0 / np.sqrt(H) / s[:, None]),
            "bv": bf(-0.5 + np.random.standard_normal(L) * 0.2),
            "eps": bf(np.random.standard_normal((B, L))),
            "Wd1": bf(np.random.standard_normal((L, H)) * 0.8 / np.sqrt(L)),
            "bd1": bf(np.random.standard_normal(H) * 0.2)}


def reference(h, Wm, bm, Wv, bv, eps, Wd1, bd1):
    hq = mxq(f64(h), 1, "e4m3")
    z_mean = (hq @ mxq(f64(Wm), 0, "e4m3")) + f64(bm)
    z_log_var = (hq @ mxq(f64(Wv), 0, "e4m3")) + f64(bv)
    z = z_mean + np.exp(0.5 * z_log_var) * f64(eps)
    hd = np.tanh((mxq(z, 1, "e4m3") @ mxq(f64(Wd1), 0, "e4m3")) + f64(bd1))
    kl = -0.5 * np.mean(z_log_var - np.square(z_mean) - np.exp(z_log_var) + 1.0)
    return hd, np.reshape(kl, (1,))

@@ -1,0 +1,222 @@
+import concourse.mybir as mybir
+from concourse.masks import make_identity
+
+F32 = mybir.dt.float32
+BF16 = mybir.dt.bfloat16
+I32 = mybir.dt.int32
+U32 = mybir.dt.uint32
+U8 = mybir.dt.uint8
+FP8X4 = mybir.dt.float8_e4m3fn_x4
+ACT = mybir.ActivationFunctionType
+ALU = mybir.AluOpType
+AXIS = mybir.AxisListType
+
+P = 128
+PACK = 4
+K_PASS = P * PACK
+N_TILE = 512
+HIDDEN = 8192
+LATENT = 512
+PASSES = HIDDEN // K_PASS
+PIECE = PACK * N_TILE
+LOAD = 4 * PIECE
+H_CHUNK = 4
+RUN = 4
+
+BD1_ROWS = HIDDEN // N_TILE
+BM_ROW = BD1_ROWS
+BV_ROW = BD1_ROWS + 1
+BIAS_ROWS = BD1_ROWS + 2
+
+FLOPS = 2 * P * HIDDEN * LATENT * 3
+
+
+def quantise_pair(nc, pools, first_piece, second_piece):
+    grouped = pools["grouped"].tile([P, 2 * PIECE], BF16, align_bytes=64)
+    places = grouped[:].rearrange("p (s c i t) -> p s c t i", s=2, i=RUN, t=PACK)
+    nc.scalar.copy(out=places[:, 0], in_=first_piece.rearrange("p t (c i) -> p c t i", i=RUN))
+    nc.vector.tensor_copy(out=places[:, 1], in_=second_piece.rearrange("p t (c i) -> p c t i", i=RUN))
+    words = pools["words"].tile([P, 2 * N_TILE], U32, align_bytes=64)
+    scales = pools["scales"].tile([P, 2 * N_TILE], U8, align_bytes=64)
+    nc.vector.quantize_mx(out=words[:].bitcast(FP8X4), scales=scales[:], in_=grouped[:])
+    return words, scales
+
+
+def tile_knowledgeawarevariationalautoencoder_pc_k_kernel(
+    tc, h, Wm, bm, Wv, bv, eps, Wd1, bd1, out_0, out_1
+):
+    nc = tc.nc
+    with (
+        tc.tile_pool(name="keep", bufs=1) as keep,
+        tc.tile_pool(name="h_stage", bufs=2) as h_stage,
+        tc.tile_pool(name="raw", bufs=5) as raw_pool,
+        tc.tile_pool(name="grouped", bufs=3) as grouped_pool,
+        tc.tile_pool(name="words", bufs=4) as words_pool,
+        tc.tile_pool(name="scales", bufs=4) as scales_pool,
+        tc.tile_pool(name="result", bufs=3) as result_pool,
+        tc.psum_pool(name="sums", bufs=1) as sums_pool,
+        tc.psum_pool(name="banks", bufs=6) as banks,
+    ):
+        pools = {"grouped": grouped_pool, "words": words_pool, "scales": scales_pool}
+
+        ident_f32 = keep.tile([P, P], F32)
+        make_identity(nc, ident_f32[:])
+        ident_bf16 = keep.tile([P, P], BF16)
+        make_identity(nc, ident_bf16[:])
+
+        bias_rows = keep.tile([P, N_TILE], BF16)
+        nc.vector.memset(bias_rows[:].bitcast(I32), 0)
+        nc.scalar.dma_start(out=bias_rows[0:BD1_ROWS, :], in_=bd1.rearrange("(r n) -> r n", n=N_TILE))
+        nc.scalar.dma_start(out=bias_rows[BM_ROW : BM_ROW + 1, :], in_=bm.rearrange("(r n) -> r n", r=1))
+        nc.scalar.dma_start(out=bias_rows[BV_ROW : BV_ROW + 1, :], in_=bv.rearrange("(r n) -> r n", r=1))
+        eps_sb = keep.tile([P, LATENT], BF16)
+        nc.scalar.dma_start(out=eps_sb[:], in_=eps)
+
+        h_words = keep.tile([P, PASSES * P], U32, align_bytes=64)
+        h_scales = keep.tile([P, PASSES * P], U8, align_bytes=64)
+        for chunk in range(PASSES // H_CHUNK):
+            h_raw = h_stage.tile([P, H_CHUNK * K_PASS], BF16, bufs=4)
+            nc.sync.dma_start(out=h_raw[:], in_=h[:, chunk * H_CHUNK * K_PASS : (chunk + 1) * H_CHUNK * K_PASS])
+            pairs = h_raw[:].bitcast(F32).rearrange("b (g p u) -> b g u p", g=H_CHUNK, u=2)
+            h_grouped = h_stage.tile([P, H_CHUNK * K_PASS], BF16, align_bytes=64)
+            h_places = h_grouped[:].bitcast(F32).rearrange("p (g b u) -> p g b u", g=H_CHUNK, u=2)
+            for half in range(H_CHUNK // 2):
+                turned = banks.tile([P, 2, 2, P], F32, tag="bank")
+                for g in range(2):
+                    for u in range(2):
+                        nc.tensor.transpose(turned[:, g, u, :], pairs[:, 2 * half + g, u, :], ident_f32[:])
+                nc.vector.tensor_copy(
+                    out=h_places[:, 2 * half : 2 * half + 2],
+                    in_=turned[:].rearrange("p g u b -> p g b u"),
+                )
+            chunk_cols = slice(chunk * H_CHUNK * P, (chunk + 1) * H_CHUNK * P)
+            nc.vector.quantize_mx(
+                out=h_words[:, chunk_cols].bitcast(FP8X4), scales=h_scales[:, chunk_cols], in_=h_grouped[:]
+            )
+
+        bias_all = keep.tile([P, BIAS_ROWS, N_TILE], BF16)
+        for r in range(0, BIAS_ROWS, 2):
+            spread = banks.tile([P, 2, N_TILE], BF16, tag="bank")
+            for j in range(2):
+                nc.tensor.matmul(
+                    spread[:, j, :],
+                    lhsT=ident_bf16[:, r + j : r + j + 1].to_broadcast([P, P]),
+                    rhs=bias_rows[:],
+                    start=True,
+                    stop=True,
+                )
+            nc.scalar.copy(out=bias_all[:, r : r + 2, :], in_=spread[:])
+
+        mean_sum = sums_pool.tile([P, LATENT], F32)
+        var_sum = sums_pool.tile([P, LATENT], F32)
+        for load in range(PASSES // 2):
+            raw = raw_pool.tile([P, 4, PIECE], BF16, tag="raw")
+            rows = slice(load * 2 * K_PASS, (load + 1) * 2 * K_PASS)
+            nc.sync.dma_start(out=raw[:, 0:2, :], in_=Wm[rows, :].rearrange("(c p t) n -> p c (t n)", c=2, t=PACK))
+            nc.sync.dma_start(out=raw[:, 2:4, :], in_=Wv[rows, :].rearrange("(c p t) n -> p c (t n)", c=2, t=PACK))
+            for s in range(2):
+                c = 2 * load + s
+                words, scales = quantise_pair(
+                    nc,
+                    pools,
+                    raw[:, s, :].rearrange("p (t n) -> p t n", t=PACK),
+                    raw[:, 2 + s, :].rearrange("p (t n) -> p t n", t=PACK),
+                )
+                for j, running_sum in enumerate((mean_sum, var_sum)):
+                    nc.tensor.matmul_mx(
+                        out=running_sum[:],
+                        lhsT=h_words[:, c * P : (c + 1) * P].bitcast(FP8X4),
+                        lhsT_scale=h_scales[:, c * P : (c + 1) * P],
+                        rhs=words[:, j * N_TILE : (j + 1) * N_TILE].bitcast(FP8X4),
+                        rhs_scale=scales[:, j * N_TILE : (j + 1) * N_TILE],
+                        start=(c == 0),
+                        stop=(c == PASSES - 1),
+                    )
+
+        z_mean = keep.tile([P, LATENT], F32)
+        nc.vector.tensor_tensor(out=z_mean[:], in0=mean_sum[:], in1=bias_all[:, BM_ROW, :], op=ALU.add)
+        z_log_var = keep.tile([P, LATENT], F32)
+        nc.vector.tensor_tensor(out=z_log_var[:], in0=var_sum[:], in1=bias_all[:, BV_ROW, :], op=ALU.add)
+        sigma = keep.tile([P, LATENT], F32)
+        nc.scalar.activation(out=sigma[:], in_=z_log_var[:], func=ACT.Exp, scale=0.5)
+        noise = keep.tile([P, LATENT], F32)
+        nc.vector.tensor_tensor(out=noise[:], in0=sigma[:], in1=eps_sb[:], op=ALU.mult)
+        z_sorted = keep.tile([P, PACK, P], BF16)
+        nc.vector.tensor_tensor(
+            out=z_sorted[:],
+            in0=z_mean[:].rearrange("b (p t) -> b t p", t=PACK),
+            in1=noise[:].rearrange("b (p t) -> b t p", t=PACK),
+            op=ALU.add,
+        )
+        z_turned = banks.tile([P, PACK, P], BF16, tag="bank")
+        for t in range(PACK):
+            nc.tensor.transpose(z_turned[:, t, :], z_sorted[:, t, :], ident_bf16[:])
+        z_grouped = keep.tile([P, P * PACK], BF16, align_bytes=64)
+        nc.vector.tensor_copy(
+            out=z_grouped[:].rearrange("p (b t) -> p b t", t=PACK),
+            in_=z_turned[:].rearrange("p t b -> p b t"),
+        )
+        z_words = keep.tile([P, P], U32, align_bytes=64)
+        z_scales = keep.tile([P, P], U8, align_bytes=64)
+        nc.vector.quantize_mx(out=z_words[:].bitcast(FP8X4), scales=z_scales[:], in_=z_grouped[:])
+
+        squares = keep.tile([P, LATENT], F32)
+        sum_squares = keep.tile([P, 1], F32)
+        nc.scalar.activation(out=squares[:], in_=z_mean[:], func=ACT.Square, accum_out=sum_squares[:])
+        variances = keep.tile([P, LATENT], F32)
+        sum_variances = keep.tile([P, 1], F32)
+        nc.scalar.activation(out=variances[:], in_=z_log_var[:], func=ACT.Exp, accum_out=sum_variances[:])
+        sum_log_var = keep.tile([P, 1], F32)
+        nc.vector.tensor_reduce(out=sum_log_var[:], in_=z_log_var[:], axis=AXIS.X, op=ALU.add)
+        row_part = keep.tile([P, 1], F32)
+        nc.vector.tensor_tensor(out=row_part[:], in0=sum_log_var[:], in1=sum_squares[:], op=ALU.subtract)
+        row_total = keep.tile([P, 1], F32)
+        nc.vector.tensor_tensor(out=row_total[:], in0=row_part[:], in1=sum_variances[:], op=ALU.subtract)
+        repeated = keep.tile([P, P], F32)
+        nc.vector.tensor_copy(out=repeated[:], in_=row_total[:, 0:1].to_broadcast([P, P]))
+        all_rows = banks.tile([P, P], F32, tag="bank")
+        nc.tensor.transpose(all_rows[:], repeated[:], ident_f32[:])
+        total = keep.tile([P, 1], F32)
+        nc.vector.tensor_reduce(out=total[:], in_=all_rows[:], axis=AXIS.X, op=ALU.add)
+        kl = keep.tile([P, 1], F32)
+        nc.vector.tensor_scalar(
+            out=kl[:], in0=total[:], scalar1=-0.5 / (P * LATENT), scalar2=-0.5, op0=ALU.mult, op1=ALU.add
+        )
+        nc.sync.dma_start(out=out_1.rearrange("(a b) -> a b", a=1), in_=kl[0:1, 0:1])
+
+        for load in range(HIDDEN * PACK // LOAD):
+            raw = raw_pool.tile([P, PACK, LOAD // PACK], BF16, tag="raw")
+            first_col = load * (LOAD // PACK)
+            nc.sync.dma_start(
+                out=raw[:],
+                in_=Wd1[:, first_col : first_col + LOAD // PACK].rearrange("(p t) n -> p t n", t=PACK),
+            )
+            for s in range(2):
+                words, scales = quantise_pair(
+                    nc,
+                    pools,
+                    raw[:, :, (2 * s) * N_TILE : (2 * s + 1) * N_TILE],
+                    raw[:, :, (2 * s + 1) * N_TILE : (2 * s + 2) * N_TILE],
+                )
+                result = result_pool.tile([P, 2, N_TILE], F32)
+                for j in range(2):
+                    product = banks.tile([P, N_TILE], F32, tag="bank")
+                    nc.tensor.matmul_mx(
+                        out=product[:],
+                        lhsT=z_words[:].bitcast(FP8X4),
+                        lhsT_scale=z_scales[:],
+                        rhs=words[:, j * N_TILE : (j + 1) * N_TILE].bitcast(FP8X4),
+                        rhs_scale=scales[:, j * N_TILE : (j + 1) * N_TILE],
+                        start=True,
+                        stop=True,
+                    )
+                    bias_row = first_col // N_TILE + 2 * s + j
+                    nc.vector.tensor_tensor(
+                        out=result[:, j, :], in0=product[:], in1=bias_all[:, bias_row, :], op=ALU.add
+                    )
+                nc.scalar.activation(out=result[:], in_=result[:], func=ACT.Tanh)
+                pair_col = first_col + 2 * s * N_TILE
+                nc.scalar.dma_start(
+                    out=out_0[:, pair_col : pair_col + 2 * N_TILE],
+                    in_=result[:].rearrange("b j n -> b (j n)"),
+                )

@@ -18,10 +18,12 @@ N_TILE = 512
 HIDDEN = 8192
 LATENT = 512
 PASSES = HIDDEN // K_PASS
+PAIRS = PASSES + HIDDEN // (2 * N_TILE)
 PIECE = PACK * N_TILE
-LOAD = 4 * PIECE
 H_CHUNK = 4
 RUN = 4
+RAW_BUFS = 8
+SEAM = 5
 
 BD1_ROWS = HIDDEN // N_TILE
 BM_ROW = BD1_ROWS
@@ -31,33 +33,84 @@ BIAS_ROWS = BD1_ROWS + 2
 FLOPS = 2 * P * HIDDEN * LATENT * 3
 
 
-def quantise_pair(nc, pools, first_piece, second_piece):
-    grouped = pools["grouped"].tile([P, 2 * PIECE], BF16, align_bytes=64)
-    places = grouped[:].rearrange("p (s c i t) -> p s c t i", s=2, i=RUN, t=PACK)
-    nc.scalar.copy(out=places[:, 0], in_=first_piece.rearrange("p t (c i) -> p c t i", i=RUN))
-    nc.vector.tensor_copy(out=places[:, 1], in_=second_piece.rearrange("p t (c i) -> p c t i", i=RUN))
-    words = pools["words"].tile([P, 2 * N_TILE], U32, align_bytes=64)
-    scales = pools["scales"].tile([P, 2 * N_TILE], U8, align_bytes=64)
-    nc.vector.quantize_mx(out=words[:].bitcast(FP8X4), scales=scales[:], in_=grouped[:])
-    return words, scales
-
-
 def tile_knowledgeawarevariationalautoencoder_pc_k_kernel(
     tc, h, Wm, bm, Wv, bv, eps, Wd1, bd1, out_0, out_1
 ):
     nc = tc.nc
     with (
         tc.tile_pool(name="keep", bufs=1) as keep,
-        tc.tile_pool(name="h_stage", bufs=2) as h_stage,
-        tc.tile_pool(name="raw", bufs=5) as raw_pool,
-        tc.tile_pool(name="grouped", bufs=3) as grouped_pool,
-        tc.tile_pool(name="words", bufs=4) as words_pool,
-        tc.tile_pool(name="scales", bufs=4) as scales_pool,
+        tc.tile_pool(name="h_raw", bufs=PASSES // H_CHUNK) as h_raw_pool,
+        tc.tile_pool(name="h_grouped", bufs=2) as h_grouped_pool,
+        tc.tile_pool(name="raw", bufs=RAW_BUFS) as raw_pool,
+        tc.tile_pool(name="grouped", bufs=4) as grouped_pool,
+        tc.tile_pool(name="quantised", bufs=SEAM + 2) as quantised_pool,
         tc.tile_pool(name="result", bufs=3) as result_pool,
         tc.psum_pool(name="sums", bufs=1) as sums_pool,
         tc.psum_pool(name="banks", bufs=6) as banks,
+        tc.manual_schedule(),
     ):
-        pools = {"grouped": grouped_pool, "words": words_pool, "scales": scales_pool}
+        h_raw_of = {}
+        h_grouped_of = {}
+        pieces_of = {}
+        grouped_of = {}
+        words_of = {}
+        scales_of = {}
+        result_of = {}
+
+
+        def load(i):
+            if i >= PAIRS:
+                return
+            if i < PASSES:
+                if i % H_CHUNK == 0:
+                    h_raw = h_raw_pool.tile([P, H_CHUNK * K_PASS], BF16)
+                    nc.sync.dma_start(out=h_raw[:], in_=h[:, i * K_PASS : (i + H_CHUNK) * K_PASS])
+                    h_raw_of[i // H_CHUNK] = h_raw
+                raw = raw_pool.tile([P, 2, PIECE], BF16, tag="raw")
+                rows = slice(i * K_PASS, (i + 1) * K_PASS)
+                nc.sync.dma_start(out=raw[:, 0, :], in_=Wm[rows, :].rearrange("(p t) n -> p (t n)", t=PACK))
+                nc.sync.dma_start(out=raw[:, 1, :], in_=Wv[rows, :].rearrange("(p t) n -> p (t n)", t=PACK))
+                by_row = raw[:].rearrange("p s (t n) -> p s t n", t=PACK)
+                pieces_of[i] = (by_row[:, 0], by_row[:, 1])
+            else:
+                raw = raw_pool.tile([P, PACK, 2 * N_TILE], BF16, tag="raw")
+                cols = slice((i - PASSES) * 2 * N_TILE, (i - PASSES + 1) * 2 * N_TILE)
+                nc.sync.dma_start(out=raw[:], in_=Wd1[:, cols].rearrange("(p t) n -> p t n", t=PACK))
+                pieces_of[i] = (raw[:, :, 0:N_TILE], raw[:, :, N_TILE : 2 * N_TILE])
+
+        def regroup(i):
+            grouped = grouped_pool.tile([P, 2 * PIECE], BF16, align_bytes=64)
+            places = grouped[:].rearrange("p (s c i t) -> p s c t i", s=2, i=RUN, t=PACK)
+            first_piece, second_piece = pieces_of[i]
+            nc.scalar.copy(out=places[:, 0], in_=first_piece.rearrange("p t (c i) -> p c t i", i=RUN))
+            nc.vector.tensor_copy(out=places[:, 1], in_=second_piece.rearrange("p t (c i) -> p c t i", i=RUN))
+            grouped_of[i] = grouped
+
+        def quantise(i):
+            words = quantised_pool.tile([P, 2 * N_TILE], U32, align_bytes=64)
+            scales = quantised_pool.tile([P, 2 * N_TILE], U8, align_bytes=64)
+            nc.vector.quantize_mx(out=words[:].bitcast(FP8X4), scales=scales[:], in_=grouped_of[i][:])
+            words_of[i] = words
+            scales_of[i] = scales
+
+        def prepare(i):
+            if i < PAIRS:
+                regroup(i)
+                load(i + RAW_BUFS)
+            if i >= 1:
+                quantise(i - 1)
+
+        def multiply(out, stationary_words, stationary_scales, i, j, start, stop):
+            nc.tensor.matmul_mx(
+                out=out,
+                lhsT=stationary_words.bitcast(FP8X4),
+                lhsT_scale=stationary_scales,
+                rhs=words_of[i][:, j * N_TILE : (j + 1) * N_TILE].bitcast(FP8X4),
+                rhs_scale=scales_of[i][:, j * N_TILE : (j + 1) * N_TILE],
+                start=start,
+                stop=stop,
+            )
+
 
         ident_f32 = keep.tile([P, P], F32)
         make_identity(nc, ident_f32[:])
@@ -72,13 +125,16 @@ def tile_knowledgeawarevariationalautoencoder_pc_k_kernel(
         eps_sb = keep.tile([P, LATENT], BF16)
         nc.scalar.dma_start(out=eps_sb[:], in_=eps)
 
+        for i in range(RAW_BUFS):
+            load(i)
+
+
         h_words = keep.tile([P, PASSES * P], U32, align_bytes=64)
         h_scales = keep.tile([P, PASSES * P], U8, align_bytes=64)
-        for chunk in range(PASSES // H_CHUNK):
-            h_raw = h_stage.tile([P, H_CHUNK * K_PASS], BF16, bufs=4)
-            nc.sync.dma_start(out=h_raw[:], in_=h[:, chunk * H_CHUNK * K_PASS : (chunk + 1) * H_CHUNK * K_PASS])
-            pairs = h_raw[:].bitcast(F32).rearrange("b (g p u) -> b g u p", g=H_CHUNK, u=2)
-            h_grouped = h_stage.tile([P, H_CHUNK * K_PASS], BF16, align_bytes=64)
+
+        def turn_h(chunk):
+            pairs = h_raw_of[chunk][:].bitcast(F32).rearrange("b (g p u) -> b g u p", g=H_CHUNK, u=2)
+            h_grouped = h_grouped_pool.tile([P, H_CHUNK * K_PASS], BF16, align_bytes=64)
             h_places = h_grouped[:].bitcast(F32).rearrange("p (g b u) -> p g b u", g=H_CHUNK, u=2)
             for half in range(H_CHUNK // 2):
                 turned = banks.tile([P, 2, 2, P], F32, tag="bank")
@@ -89,13 +145,19 @@ def tile_knowledgeawarevariationalautoencoder_pc_k_kernel(
                     out=h_places[:, 2 * half : 2 * half + 2],
                     in_=turned[:].rearrange("p g u b -> p g b u"),
                 )
+            h_grouped_of[chunk] = h_grouped
+
+        def quantise_h(chunk):
             chunk_cols = slice(chunk * H_CHUNK * P, (chunk + 1) * H_CHUNK * P)
             nc.vector.quantize_mx(
-                out=h_words[:, chunk_cols].bitcast(FP8X4), scales=h_scales[:, chunk_cols], in_=h_grouped[:]
+                out=h_words[:, chunk_cols].bitcast(FP8X4),
+                scales=h_scales[:, chunk_cols],
+                in_=h_grouped_of[chunk][:],
             )
 
         bias_all = keep.tile([P, BIAS_ROWS, N_TILE], BF16)
-        for r in range(0, BIAS_ROWS, 2):
+
+        def spread_bias(r):
             spread = banks.tile([P, 2, N_TILE], BF16, tag="bank")
             for j in range(2):
                 nc.tensor.matmul(
@@ -109,36 +171,47 @@ def tile_knowledgeawarevariationalautoencoder_pc_k_kernel(
 
         mean_sum = sums_pool.tile([P, LATENT], F32)
         var_sum = sums_pool.tile([P, LATENT], F32)
-        for load in range(PASSES // 2):
-            raw = raw_pool.tile([P, 4, PIECE], BF16, tag="raw")
-            rows = slice(load * 2 * K_PASS, (load + 1) * 2 * K_PASS)
-            nc.sync.dma_start(out=raw[:, 0:2, :], in_=Wm[rows, :].rearrange("(c p t) n -> p c (t n)", c=2, t=PACK))
-            nc.sync.dma_start(out=raw[:, 2:4, :], in_=Wv[rows, :].rearrange("(c p t) n -> p c (t n)", c=2, t=PACK))
-            for s in range(2):
-                c = 2 * load + s
-                words, scales = quantise_pair(
-                    nc,
-                    pools,
-                    raw[:, s, :].rearrange("p (t n) -> p t n", t=PACK),
-                    raw[:, 2 + s, :].rearrange("p (t n) -> p t n", t=PACK),
+
+        def multiply_first(c):
+            for j, running_sum in enumerate((mean_sum, var_sum)):
+                multiply(
+                    running_sum[:],
+                    h_words[:, c * P : (c + 1) * P],
+                    h_scales[:, c * P : (c + 1) * P],
+                    c,
+                    j,
+                    start=(c == 0),
+                    stop=(c == PASSES - 1),
                 )
-                for j, running_sum in enumerate((mean_sum, var_sum)):
-                    nc.tensor.matmul_mx(
-                        out=running_sum[:],
-                        lhsT=h_words[:, c * P : (c + 1) * P].bitcast(FP8X4),
-                        lhsT_scale=h_scales[:, c * P : (c + 1) * P],
-                        rhs=words[:, j * N_TILE : (j + 1) * N_TILE].bitcast(FP8X4),
-                        rhs_scale=scales[:, j * N_TILE : (j + 1) * N_TILE],
-                        start=(c == 0),
-                        stop=(c == PASSES - 1),
-                    )
+
+        for i in range(PASSES + 2):
+            if i < PASSES and i % H_CHUNK == 0:
+                turn_h(i // H_CHUNK)
+            if i < PASSES and i % H_CHUNK == 1:
+                quantise_h(i // H_CHUNK)
+            prepare(i)
+            if i % 2 == 0:
+                spread_bias(i)
+            if i >= 2:
+                multiply_first(i - 2)
+
 
         z_mean = keep.tile([P, LATENT], F32)
         nc.vector.tensor_tensor(out=z_mean[:], in0=mean_sum[:], in1=bias_all[:, BM_ROW, :], op=ALU.add)
         z_log_var = keep.tile([P, LATENT], F32)
         nc.vector.tensor_tensor(out=z_log_var[:], in0=var_sum[:], in1=bias_all[:, BV_ROW, :], op=ALU.add)
+
+        prepare(PASSES + 2)
+
         sigma = keep.tile([P, LATENT], F32)
         nc.scalar.activation(out=sigma[:], in_=z_log_var[:], func=ACT.Exp, scale=0.5)
+        squares = keep.tile([P, LATENT], F32)
+        sum_squares = keep.tile([P, 1], F32)
+        nc.scalar.activation(out=squares[:], in_=z_mean[:], func=ACT.Square, accum_out=sum_squares[:])
+        variances = keep.tile([P, LATENT], F32)
+        sum_variances = keep.tile([P, 1], F32)
+        nc.scalar.activation(out=variances[:], in_=z_log_var[:], func=ACT.Exp, accum_out=sum_variances[:])
+
         noise = keep.tile([P, LATENT], F32)
         nc.vector.tensor_tensor(out=noise[:], in0=sigma[:], in1=eps_sb[:], op=ALU.mult)
         z_sorted = keep.tile([P, PACK, P], BF16)
@@ -151,23 +224,16 @@ def tile_knowledgeawarevariationalautoencoder_pc_k_kernel(
         z_turned = banks.tile([P, PACK, P], BF16, tag="bank")
         for t in range(PACK):
             nc.tensor.transpose(z_turned[:, t, :], z_sorted[:, t, :], ident_bf16[:])
+        sum_log_var = keep.tile([P, 1], F32)
+        nc.vector.tensor_reduce(out=sum_log_var[:], in_=z_log_var[:], axis=AXIS.X, op=ALU.add)
+
+        prepare(PASSES + 3)
+
         z_grouped = keep.tile([P, P * PACK], BF16, align_bytes=64)
         nc.vector.tensor_copy(
             out=z_grouped[:].rearrange("p (b t) -> p b t", t=PACK),
             in_=z_turned[:].rearrange("p t b -> p b t"),
         )
-        z_words = keep.tile([P, P], U32, align_bytes=64)
-        z_scales = keep.tile([P, P], U8, align_bytes=64)
-        nc.vector.quantize_mx(out=z_words[:].bitcast(FP8X4), scales=z_scales[:], in_=z_grouped[:])
-
-        squares = keep.tile([P, LATENT], F32)
-        sum_squares = keep.tile([P, 1], F32)
-        nc.scalar.activation(out=squares[:], in_=z_mean[:], func=ACT.Square, accum_out=sum_squares[:])
-        variances = keep.tile([P, LATENT], F32)
-        sum_variances = keep.tile([P, 1], F32)
-        nc.scalar.activation(out=variances[:], in_=z_log_var[:], func=ACT.Exp, accum_out=sum_variances[:])
-        sum_log_var = keep.tile([P, 1], F32)
-        nc.vector.tensor_reduce(out=sum_log_var[:], in_=z_log_var[:], axis=AXIS.X, op=ALU.add)
         row_part = keep.tile([P, 1], F32)
         nc.vector.tensor_tensor(out=row_part[:], in0=sum_log_var[:], in1=sum_squares[:], op=ALU.subtract)
         row_total = keep.tile([P, 1], F32)
@@ -176,47 +242,41 @@ def tile_knowledgeawarevariationalautoencoder_pc_k_kernel(
         nc.vector.tensor_copy(out=repeated[:], in_=row_total[:, 0:1].to_broadcast([P, P]))
         all_rows = banks.tile([P, P], F32, tag="bank")
         nc.tensor.transpose(all_rows[:], repeated[:], ident_f32[:])
-        total = keep.tile([P, 1], F32)
-        nc.vector.tensor_reduce(out=total[:], in_=all_rows[:], axis=AXIS.X, op=ALU.add)
+
+        prepare(PASSES + 4)
+
+        z_words = keep.tile([P, P], U32, align_bytes=64)
+        z_scales = keep.tile([P, P], U8, align_bytes=64)
+        nc.vector.quantize_mx(out=z_words[:].bitcast(FP8X4), scales=z_scales[:], in_=z_grouped[:])
+        grand_total = keep.tile([P, 1], F32)
+        nc.vector.tensor_reduce(out=grand_total[:], in_=all_rows[:], axis=AXIS.X, op=ALU.add)
         kl = keep.tile([P, 1], F32)
         nc.vector.tensor_scalar(
-            out=kl[:], in0=total[:], scalar1=-0.5 / (P * LATENT), scalar2=-0.5, op0=ALU.mult, op1=ALU.add
+            out=kl[:], in0=grand_total[:], scalar1=-0.5 / (P * LATENT), scalar2=-0.5, op0=ALU.mult, op1=ALU.add
         )
         nc.sync.dma_start(out=out_1.rearrange("(a b) -> a b", a=1), in_=kl[0:1, 0:1])
 
-        for load in range(HIDDEN * PACK // LOAD):
-            raw = raw_pool.tile([P, PACK, LOAD // PACK], BF16, tag="raw")
-            first_col = load * (LOAD // PACK)
-            nc.sync.dma_start(
-                out=raw[:],
-                in_=Wd1[:, first_col : first_col + LOAD // PACK].rearrange("(p t) n -> p t n", t=PACK),
-            )
-            for s in range(2):
-                words, scales = quantise_pair(
-                    nc,
-                    pools,
-                    raw[:, :, (2 * s) * N_TILE : (2 * s + 1) * N_TILE],
-                    raw[:, :, (2 * s + 1) * N_TILE : (2 * s + 2) * N_TILE],
+
+        def project(i):
+            result = result_pool.tile([P, 2, N_TILE], F32)
+            for j in range(2):
+                product = banks.tile([P, N_TILE], F32, tag="bank")
+                multiply(product[:], z_words[:], z_scales[:], i, j, start=True, stop=True)
+                nc.vector.tensor_tensor(
+                    out=result[:, j, :], in0=product[:], in1=bias_all[:, 2 * (i - PASSES) + j, :], op=ALU.add
                 )
-                result = result_pool.tile([P, 2, N_TILE], F32)
-                for j in range(2):
-                    product = banks.tile([P, N_TILE], F32, tag="bank")
-                    nc.tensor.matmul_mx(
-                        out=product[:],
-                        lhsT=z_words[:].bitcast(FP8X4),
-                        lhsT_scale=z_scales[:],
-                        rhs=words[:, j * N_TILE : (j + 1) * N_TILE].bitcast(FP8X4),
-                        rhs_scale=scales[:, j * N_TILE : (j + 1) * N_TILE],
-                        start=True,
-                        stop=True,
-                    )
-                    bias_row = first_col // N_TILE + 2 * s + j
-                    nc.vector.tensor_tensor(
-                        out=result[:, j, :], in0=product[:], in1=bias_all[:, bias_row, :], op=ALU.add
-                    )
-                nc.scalar.activation(out=result[:], in_=result[:], func=ACT.Tanh)
-                pair_col = first_col + 2 * s * N_TILE
-                nc.scalar.dma_start(
-                    out=out_0[:, pair_col : pair_col + 2 * N_TILE],
-                    in_=result[:].rearrange("b j n -> b (j n)"),
-                )
+            result_of[i] = result
+
+        def squash(i):
+            result = result_of[i]
+            nc.scalar.activation(out=result[:], in_=result[:], func=ACT.Tanh)
+            cols = slice((i - PASSES) * 2 * N_TILE, (i - PASSES + 1) * 2 * N_TILE)
+            nc.scalar.dma_start(out=out_0[:, cols], in_=result[:].rearrange("b j n -> b (j n)"))
+
+        for i in range(PASSES + SEAM, PAIRS + SEAM + 1):
+            if i <= PAIRS:
+                prepare(i)
+            if i - SEAM < PAIRS:
+                project(i - SEAM)
+            if i - SEAM - 1 >= PASSES:
+                squash(i - SEAM - 1)

@@ -3,7 +3,6 @@ from concourse.masks import make_identity
 
 F32 = mybir.dt.float32
 BF16 = mybir.dt.bfloat16
-I32 = mybir.dt.int32
 U32 = mybir.dt.uint32
 U8 = mybir.dt.uint8
 FP8X4 = mybir.dt.float8_e4m3fn_x4
@@ -23,12 +22,8 @@ PIECE = PACK * N_TILE
 H_CHUNK = 4
 RUN = 4
 RAW_BUFS = 8
+SCALAR_COLS = 608
 SEAM = 5
-
-BD1_ROWS = HIDDEN // N_TILE
-BM_ROW = BD1_ROWS
-BV_ROW = BD1_ROWS + 1
-BIAS_ROWS = BD1_ROWS + 2
 
 FLOPS = 2 * P * HIDDEN * LATENT * 3
 
@@ -44,7 +39,7 @@ def tile_knowledgeawarevariationalautoencoder_pc_k_kernel(
         tc.tile_pool(name="raw", bufs=RAW_BUFS) as raw_pool,
         tc.tile_pool(name="grouped", bufs=4) as grouped_pool,
         tc.tile_pool(name="quantised", bufs=SEAM + 2) as quantised_pool,
-        tc.tile_pool(name="result", bufs=3) as result_pool,
+        tc.tile_pool(name="result", bufs=5) as result_pool,
         tc.psum_pool(name="sums", bufs=1) as sums_pool,
         tc.psum_pool(name="banks", bufs=6) as banks,
         tc.manual_schedule(),
@@ -60,7 +55,13 @@ def tile_knowledgeawarevariationalautoencoder_pc_k_kernel(
 
         def load(i):
             if i >= PAIRS:
+                if i == PAIRS:
+                    nc.sync.dma_start(out=out_bias[:], in_=bd1.partition_broadcast(P))
                 return
+            if i == PASSES:
+                nc.sync.dma_start(out=mean_bias[:], in_=bm.partition_broadcast(P))
+                nc.sync.dma_start(out=var_bias[:], in_=bv.partition_broadcast(P))
+                nc.sync.dma_start(out=eps_sb[:], in_=eps)
             if i < PASSES:
                 if i % H_CHUNK == 0:
                     h_raw = h_raw_pool.tile([P, H_CHUNK * K_PASS], BF16)
@@ -76,14 +77,16 @@ def tile_knowledgeawarevariationalautoencoder_pc_k_kernel(
                 raw = raw_pool.tile([P, PACK, 2 * N_TILE], BF16, tag="raw")
                 cols = slice((i - PASSES) * 2 * N_TILE, (i - PASSES + 1) * 2 * N_TILE)
                 nc.sync.dma_start(out=raw[:], in_=Wd1[:, cols].rearrange("(p t) n -> p t n", t=PACK))
-                pieces_of[i] = (raw[:, :, 0:N_TILE], raw[:, :, N_TILE : 2 * N_TILE])
+                pieces_of[i] = (raw[:, :, 0:SCALAR_COLS], raw[:, :, SCALAR_COLS : 2 * N_TILE])
 
         def regroup(i):
             grouped = grouped_pool.tile([P, 2 * PIECE], BF16, align_bytes=64)
-            places = grouped[:].rearrange("p (s c i t) -> p s c t i", s=2, i=RUN, t=PACK)
             first_piece, second_piece = pieces_of[i]
-            nc.scalar.copy(out=places[:, 0], in_=first_piece.rearrange("p t (c i) -> p c t i", i=RUN))
-            nc.vector.tensor_copy(out=places[:, 1], in_=second_piece.rearrange("p t (c i) -> p c t i", i=RUN))
+            split = first_piece.shape[2]
+            first_places = grouped[:, : split * PACK].rearrange("p (c i t) -> p c t i", i=RUN, t=PACK)
+            second_places = grouped[:, split * PACK :].rearrange("p (c i t) -> p c t i", i=RUN, t=PACK)
+            nc.scalar.copy(out=first_places, in_=first_piece.rearrange("p t (c i) -> p c t i", i=RUN))
+            nc.vector.tensor_copy(out=second_places, in_=second_piece.rearrange("p t (c i) -> p c t i", i=RUN))
             grouped_of[i] = grouped
 
         def quantise(i):
@@ -117,13 +120,10 @@ def tile_knowledgeawarevariationalautoencoder_pc_k_kernel(
         ident_bf16 = keep.tile([P, P], BF16)
         make_identity(nc, ident_bf16[:])
 
-        bias_rows = keep.tile([P, N_TILE], BF16)
-        nc.vector.memset(bias_rows[:].bitcast(I32), 0)
-        nc.scalar.dma_start(out=bias_rows[0:BD1_ROWS, :], in_=bd1.rearrange("(r n) -> r n", n=N_TILE))
-        nc.scalar.dma_start(out=bias_rows[BM_ROW : BM_ROW + 1, :], in_=bm.rearrange("(r n) -> r n", r=1))
-        nc.scalar.dma_start(out=bias_rows[BV_ROW : BV_ROW + 1, :], in_=bv.rearrange("(r n) -> r n", r=1))
         eps_sb = keep.tile([P, LATENT], BF16)
-        nc.scalar.dma_start(out=eps_sb[:], in_=eps)
+        mean_bias = keep.tile([P, LATENT], BF16)
+        var_bias = keep.tile([P, LATENT], BF16)
+        out_bias = keep.tile([P, HIDDEN], BF16)
 
         for i in range(RAW_BUFS):
             load(i)
@@ -141,7 +141,7 @@ def tile_knowledgeawarevariationalautoencoder_pc_k_kernel(
                 for g in range(2):
                     for u in range(2):
                         nc.tensor.transpose(turned[:, g, u, :], pairs[:, 2 * half + g, u, :], ident_f32[:])
-                nc.vector.tensor_copy(
+                nc.scalar.copy(
                     out=h_places[:, 2 * half : 2 * half + 2],
                     in_=turned[:].rearrange("p g u b -> p g b u"),
                 )
@@ -154,20 +154,6 @@ def tile_knowledgeawarevariationalautoencoder_pc_k_kernel(
                 scales=h_scales[:, chunk_cols],
                 in_=h_grouped_of[chunk][:],
             )
-
-        bias_all = keep.tile([P, BIAS_ROWS, N_TILE], BF16)
-
-        def spread_bias(r):
-            spread = banks.tile([P, 2, N_TILE], BF16, tag="bank")
-            for j in range(2):
-                nc.tensor.matmul(
-                    spread[:, j, :],
-                    lhsT=ident_bf16[:, r + j : r + j + 1].to_broadcast([P, P]),
-                    rhs=bias_rows[:],
-                    start=True,
-                    stop=True,
-                )
-            nc.scalar.copy(out=bias_all[:, r : r + 2, :], in_=spread[:])
 
         mean_sum = sums_pool.tile([P, LATENT], F32)
         var_sum = sums_pool.tile([P, LATENT], F32)
@@ -190,16 +176,14 @@ def tile_knowledgeawarevariationalautoencoder_pc_k_kernel(
             if i < PASSES and i % H_CHUNK == 1:
                 quantise_h(i // H_CHUNK)
             prepare(i)
-            if i % 2 == 0:
-                spread_bias(i)
             if i >= 2:
                 multiply_first(i - 2)
 
 
         z_mean = keep.tile([P, LATENT], F32)
-        nc.vector.tensor_tensor(out=z_mean[:], in0=mean_sum[:], in1=bias_all[:, BM_ROW, :], op=ALU.add)
+        nc.vector.tensor_tensor(out=z_mean[:], in0=mean_sum[:], in1=mean_bias[:], op=ALU.add)
         z_log_var = keep.tile([P, LATENT], F32)
-        nc.vector.tensor_tensor(out=z_log_var[:], in0=var_sum[:], in1=bias_all[:, BV_ROW, :], op=ALU.add)
+        nc.vector.tensor_tensor(out=z_log_var[:], in0=var_sum[:], in1=var_bias[:], op=ALU.add)
 
         prepare(PASSES + 2)
 
@@ -262,8 +246,9 @@ def tile_knowledgeawarevariationalautoencoder_pc_k_kernel(
             for j in range(2):
                 product = banks.tile([P, N_TILE], F32, tag="bank")
                 multiply(product[:], z_words[:], z_scales[:], i, j, start=True, stop=True)
+                first = (2 * (i - PASSES) + j) * N_TILE
                 nc.vector.tensor_tensor(
-                    out=result[:, j, :], in0=product[:], in1=bias_all[:, 2 * (i - PASSES) + j, :], op=ALU.add
+                    out=result[:, j, :], in0=product[:], in1=out_bias[:, first : first + N_TILE], op=ALU.add
                 )
             result_of[i] = result
 
@@ -273,10 +258,15 @@ def tile_knowledgeawarevariationalautoencoder_pc_k_kernel(
             cols = slice((i - PASSES) * 2 * N_TILE, (i - PASSES + 1) * 2 * N_TILE)
             nc.scalar.dma_start(out=out_0[:, cols], in_=result[:].rearrange("b j n -> b (j n)"))
 
-        for i in range(PASSES + SEAM, PAIRS + SEAM + 1):
+        projected = PASSES
+        squashed = PASSES
+        for i in range(PASSES + SEAM, PAIRS + 3):
             if i <= PAIRS:
                 prepare(i)
-            if i - SEAM < PAIRS:
-                project(i - SEAM)
-            if i - SEAM - 1 >= PASSES:
-                squash(i - SEAM - 1)
+            ready = projected
+            for j in range(projected, min(projected + 2, i - 1, PAIRS)):
+                project(j)
+                projected = j + 1
+            for j in range(squashed, ready):
+                squash(j)
+                squashed = j + 1

@@ -3,12 +3,12 @@ from concourse.masks import make_identity
 
 F32 = mybir.dt.float32
 BF16 = mybir.dt.bfloat16
+I32 = mybir.dt.int32
 U32 = mybir.dt.uint32
 U8 = mybir.dt.uint8
 FP8X4 = mybir.dt.float8_e4m3fn_x4
 ACT = mybir.ActivationFunctionType
 ALU = mybir.AluOpType
-AXIS = mybir.AxisListType
 
 P = 128
 PACK = 4
@@ -19,11 +19,20 @@ LATENT = 512
 PASSES = HIDDEN // K_PASS
 PAIRS = PASSES + HIDDEN // (2 * N_TILE)
 PIECE = PACK * N_TILE
-H_CHUNK = 4
+H_CHUNK = 2
 RUN = 4
 RAW_BUFS = 8
-SCALAR_COLS = 608
+SCALAR_COLS = 512
 SEAM = 5
+
+BD1_ROWS = HIDDEN // N_TILE
+BM_ROW = BD1_ROWS
+BV_ROW = BD1_ROWS + 1
+BIAS_ROWS = BD1_ROWS + 2
+SMALL_BEFORE = 5
+FIRST_SPREAD = 8
+
+KL_FACTOR = 0.5 / (P * LATENT)
 
 FLOPS = 2 * P * HIDDEN * LATENT * 3
 
@@ -55,24 +64,24 @@ def tile_knowledgeawarevariationalautoencoder_pc_k_kernel(
 
         def load(i):
             if i >= PAIRS:
-                if i == PAIRS:
-                    nc.sync.dma_start(out=out_bias[:], in_=bd1.partition_broadcast(P))
                 return
-            if i == PASSES:
-                nc.sync.dma_start(out=mean_bias[:], in_=bm.partition_broadcast(P))
-                nc.sync.dma_start(out=var_bias[:], in_=bv.partition_broadcast(P))
+            if i == SMALL_BEFORE:
+                nc.sync.dma_start(out=bias_rows[0:BD1_ROWS, :], in_=bd1.rearrange("(r n) -> r n", n=N_TILE))
+                nc.sync.dma_start(out=bias_rows[BM_ROW : BM_ROW + 1, :], in_=bm.rearrange("(r n) -> r n", r=1))
+                nc.sync.dma_start(out=bias_rows[BV_ROW : BV_ROW + 1, :], in_=bv.rearrange("(r n) -> r n", r=1))
                 nc.sync.dma_start(out=eps_sb[:], in_=eps)
             if i < PASSES:
-                if i % H_CHUNK == 0:
-                    h_raw = h_raw_pool.tile([P, H_CHUNK * K_PASS], BF16)
-                    nc.sync.dma_start(out=h_raw[:], in_=h[:, i * K_PASS : (i + H_CHUNK) * K_PASS])
-                    h_raw_of[i // H_CHUNK] = h_raw
                 raw = raw_pool.tile([P, 2, PIECE], BF16, tag="raw")
                 rows = slice(i * K_PASS, (i + 1) * K_PASS)
                 nc.sync.dma_start(out=raw[:, 0, :], in_=Wm[rows, :].rearrange("(p t) n -> p (t n)", t=PACK))
                 nc.sync.dma_start(out=raw[:, 1, :], in_=Wv[rows, :].rearrange("(p t) n -> p (t n)", t=PACK))
                 by_row = raw[:].rearrange("p s (t n) -> p s t n", t=PACK)
                 pieces_of[i] = (by_row[:, 0], by_row[:, 1])
+                if i % H_CHUNK == H_CHUNK - 1:
+                    chunk = i // H_CHUNK
+                    h_raw = h_raw_pool.tile([P, H_CHUNK * K_PASS], BF16)
+                    nc.sync.dma_start(out=h_raw[:], in_=h[:, chunk * H_CHUNK * K_PASS : (chunk + 1) * H_CHUNK * K_PASS])
+                    h_raw_of[chunk] = h_raw
             else:
                 raw = raw_pool.tile([P, PACK, 2 * N_TILE], BF16, tag="raw")
                 cols = slice((i - PASSES) * 2 * N_TILE, (i - PASSES + 1) * 2 * N_TILE)
@@ -82,6 +91,15 @@ def tile_knowledgeawarevariationalautoencoder_pc_k_kernel(
         def regroup(i):
             grouped = grouped_pool.tile([P, 2 * PIECE], BF16, align_bytes=64)
             first_piece, second_piece = pieces_of[i]
+            if i == 0:
+                for s, piece in enumerate((first_piece, second_piece)):
+                    places = grouped[:, s * PIECE : (s + 1) * PIECE].rearrange("p (c i t) -> p c t i", i=RUN, t=PACK)
+                    source = piece.rearrange("p t (c i) -> p c t i", i=RUN)
+                    middle = N_TILE // RUN // 2
+                    nc.scalar.copy(out=places[:, :middle], in_=source[:, :middle])
+                    nc.vector.tensor_copy(out=places[:, middle:], in_=source[:, middle:])
+                grouped_of[i] = grouped
+                return
             split = first_piece.shape[2]
             first_places = grouped[:, : split * PACK].rearrange("p (c i t) -> p c t i", i=RUN, t=PACK)
             second_places = grouped[:, split * PACK :].rearrange("p (c i t) -> p c t i", i=RUN, t=PACK)
@@ -119,11 +137,14 @@ def tile_knowledgeawarevariationalautoencoder_pc_k_kernel(
         make_identity(nc, ident_f32[:])
         ident_bf16 = keep.tile([P, P], BF16)
         make_identity(nc, ident_bf16[:])
+        minus_factor = keep.tile([P, P], F32)
+        nc.gpsimd.memset(minus_factor[:], -KL_FACTOR)
+        plus_factor = keep.tile([P, P], F32)
+        nc.gpsimd.memset(plus_factor[:], KL_FACTOR)
 
+        bias_rows = keep.tile([P, N_TILE], BF16)
+        nc.vector.memset(bias_rows[:].bitcast(I32), 0)
         eps_sb = keep.tile([P, LATENT], BF16)
-        mean_bias = keep.tile([P, LATENT], BF16)
-        var_bias = keep.tile([P, LATENT], BF16)
-        out_bias = keep.tile([P, HIDDEN], BF16)
 
         for i in range(RAW_BUFS):
             load(i)
@@ -136,15 +157,11 @@ def tile_knowledgeawarevariationalautoencoder_pc_k_kernel(
             pairs = h_raw_of[chunk][:].bitcast(F32).rearrange("b (g p u) -> b g u p", g=H_CHUNK, u=2)
             h_grouped = h_grouped_pool.tile([P, H_CHUNK * K_PASS], BF16, align_bytes=64)
             h_places = h_grouped[:].bitcast(F32).rearrange("p (g b u) -> p g b u", g=H_CHUNK, u=2)
-            for half in range(H_CHUNK // 2):
-                turned = banks.tile([P, 2, 2, P], F32, tag="bank")
-                for g in range(2):
-                    for u in range(2):
-                        nc.tensor.transpose(turned[:, g, u, :], pairs[:, 2 * half + g, u, :], ident_f32[:])
-                nc.scalar.copy(
-                    out=h_places[:, 2 * half : 2 * half + 2],
-                    in_=turned[:].rearrange("p g u b -> p g b u"),
-                )
+            turned = banks.tile([P, H_CHUNK, 2, P], F32, tag="bank")
+            for g in range(H_CHUNK):
+                for u in range(2):
+                    nc.tensor.transpose(turned[:, g, u, :], pairs[:, g, u, :], ident_f32[:])
+            nc.scalar.copy(out=h_places, in_=turned[:].rearrange("p g u b -> p g b u"))
             h_grouped_of[chunk] = h_grouped
 
         def quantise_h(chunk):
@@ -154,6 +171,20 @@ def tile_knowledgeawarevariationalautoencoder_pc_k_kernel(
                 scales=h_scales[:, chunk_cols],
                 in_=h_grouped_of[chunk][:],
             )
+
+        bias_all = keep.tile([P, BIAS_ROWS, N_TILE], BF16)
+
+        def spread_bias(r):
+            spread = banks.tile([P, 2, N_TILE], BF16, tag="bank")
+            for j in range(2):
+                nc.tensor.matmul(
+                    spread[:, j, :],
+                    lhsT=ident_bf16[:, r + j : r + j + 1].to_broadcast([P, P]),
+                    rhs=bias_rows[:],
+                    start=True,
+                    stop=True,
+                )
+            nc.scalar.copy(out=bias_all[:, r : r + 2, :], in_=spread[:])
 
         mean_sum = sums_pool.tile([P, LATENT], F32)
         var_sum = sums_pool.tile([P, LATENT], F32)
@@ -171,19 +202,32 @@ def tile_knowledgeawarevariationalautoencoder_pc_k_kernel(
                 )
 
         for i in range(PASSES + 2):
-            if i < PASSES and i % H_CHUNK == 0:
-                turn_h(i // H_CHUNK)
-            if i < PASSES and i % H_CHUNK == 1:
-                quantise_h(i // H_CHUNK)
             prepare(i)
-            if i >= 2:
-                multiply_first(i - 2)
+            if i < PASSES and i % H_CHUNK == H_CHUNK - 1:
+                turn_h(i // H_CHUNK)
+            if 1 <= i <= PASSES and (i - 1) % H_CHUNK == H_CHUNK - 1:
+                quantise_h((i - 1) // H_CHUNK)
+            if i % H_CHUNK == H_CHUNK - 1 and i > H_CHUNK:
+                for c in range(i - 1 - H_CHUNK, i - 1):
+                    multiply_first(c)
+            r = 2 * (i - FIRST_SPREAD)
+            if 0 <= r < BIAS_ROWS:
+                spread_bias(r)
 
 
         z_mean = keep.tile([P, LATENT], F32)
-        nc.vector.tensor_tensor(out=z_mean[:], in0=mean_sum[:], in1=mean_bias[:], op=ALU.add)
+        nc.vector.tensor_tensor(out=z_mean[:], in0=mean_sum[:], in1=bias_all[:, BM_ROW, :], op=ALU.add)
         z_log_var = keep.tile([P, LATENT], F32)
-        nc.vector.tensor_tensor(out=z_log_var[:], in0=var_sum[:], in1=var_bias[:], op=ALU.add)
+        sum_log_var = keep.tile([P, 1], F32)
+        nc.vector.scalar_tensor_tensor(
+            out=z_log_var[:],
+            in0=var_sum[:],
+            scalar=1.0,
+            in1=bias_all[:, BV_ROW, :],
+            op0=ALU.mult,
+            op1=ALU.add,
+            accum_out=sum_log_var[:],
+        )
 
         prepare(PASSES + 2)
 
@@ -208,8 +252,6 @@ def tile_knowledgeawarevariationalautoencoder_pc_k_kernel(
         z_turned = banks.tile([P, PACK, P], BF16, tag="bank")
         for t in range(PACK):
             nc.tensor.transpose(z_turned[:, t, :], z_sorted[:, t, :], ident_bf16[:])
-        sum_log_var = keep.tile([P, 1], F32)
-        nc.vector.tensor_reduce(out=sum_log_var[:], in_=z_log_var[:], axis=AXIS.X, op=ALU.add)
 
         prepare(PASSES + 3)
 
@@ -218,26 +260,19 @@ def tile_knowledgeawarevariationalautoencoder_pc_k_kernel(
             out=z_grouped[:].rearrange("p (b t) -> p b t", t=PACK),
             in_=z_turned[:].rearrange("p t b -> p b t"),
         )
-        row_part = keep.tile([P, 1], F32)
-        nc.vector.tensor_tensor(out=row_part[:], in0=sum_log_var[:], in1=sum_squares[:], op=ALU.subtract)
-        row_total = keep.tile([P, 1], F32)
-        nc.vector.tensor_tensor(out=row_total[:], in0=row_part[:], in1=sum_variances[:], op=ALU.subtract)
-        repeated = keep.tile([P, P], F32)
-        nc.vector.tensor_copy(out=repeated[:], in_=row_total[:, 0:1].to_broadcast([P, P]))
-        all_rows = banks.tile([P, P], F32, tag="bank")
-        nc.tensor.transpose(all_rows[:], repeated[:], ident_f32[:])
+        kl_sum = banks.tile([P, 1], F32, tag="bank")
+        for n, (factor, row_sums) in enumerate(
+            ((minus_factor, sum_log_var), (plus_factor, sum_squares), (plus_factor, sum_variances))
+        ):
+            nc.tensor.matmul(kl_sum[:], lhsT=factor[:], rhs=row_sums[:], start=(n == 0), stop=(n == 2))
 
         prepare(PASSES + 4)
 
         z_words = keep.tile([P, P], U32, align_bytes=64)
         z_scales = keep.tile([P, P], U8, align_bytes=64)
         nc.vector.quantize_mx(out=z_words[:].bitcast(FP8X4), scales=z_scales[:], in_=z_grouped[:])
-        grand_total = keep.tile([P, 1], F32)
-        nc.vector.tensor_reduce(out=grand_total[:], in_=all_rows[:], axis=AXIS.X, op=ALU.add)
         kl = keep.tile([P, 1], F32)
-        nc.vector.tensor_scalar(
-            out=kl[:], in0=grand_total[:], scalar1=-0.5 / (P * LATENT), scalar2=-0.5, op0=ALU.mult, op1=ALU.add
-        )
+        nc.vector.tensor_scalar_add(out=kl[:], in0=kl_sum[:], scalar1=-0.5)
         nc.sync.dma_start(out=out_1.rearrange("(a b) -> a b", a=1), in_=kl[0:1, 0:1])
 
 
@@ -246,9 +281,8 @@ def tile_knowledgeawarevariationalautoencoder_pc_k_kernel(
             for j in range(2):
                 product = banks.tile([P, N_TILE], F32, tag="bank")
                 multiply(product[:], z_words[:], z_scales[:], i, j, start=True, stop=True)
-                first = (2 * (i - PASSES) + j) * N_TILE
                 nc.vector.tensor_tensor(
-                    out=result[:, j, :], in0=product[:], in1=out_bias[:, first : first + N_TILE], op=ALU.add
+                    out=result[:, j, :], in0=product[:], in1=bias_all[:, 2 * (i - PASSES) + j, :], op=ALU.add
                 )
             result_of[i] = result
 

@@ -20,7 +20,7 @@ PASSES = HIDDEN // K_PASS
 PAIRS = PASSES + HIDDEN // (2 * N_TILE)
 PIECE = PACK * N_TILE
 H_CHUNK = 2
-RUN = 4
+RUN = 8
 RAW_BUFS = 8
 SCALAR_COLS = 512
 SEAM = 5

@@ -22,7 +22,8 @@ PIECE = PACK * N_TILE
 H_CHUNK = 2
 RUN = 8
 RAW_BUFS = 8
-SCALAR_COLS = 512
+SCALAR_COLS_FIRST = 384
+SCALAR_COLS = 480
 SEAM = 5
 
 BD1_ROWS = HIDDEN // N_TILE
@@ -86,25 +87,31 @@ def tile_knowledgeawarevariationalautoencoder_pc_k_kernel(
                 raw = raw_pool.tile([P, PACK, 2 * N_TILE], BF16, tag="raw")
                 cols = slice((i - PASSES) * 2 * N_TILE, (i - PASSES + 1) * 2 * N_TILE)
                 nc.sync.dma_start(out=raw[:], in_=Wd1[:, cols].rearrange("(p t) n -> p t n", t=PACK))
-                pieces_of[i] = (raw[:, :, 0:SCALAR_COLS], raw[:, :, SCALAR_COLS : 2 * N_TILE])
+                pieces_of[i] = (raw[:],)
 
         def regroup(i):
             grouped = grouped_pool.tile([P, 2 * PIECE], BF16, align_bytes=64)
-            first_piece, second_piece = pieces_of[i]
+            places = grouped[:].rearrange("p (c i t) -> p c t i", i=RUN, t=PACK)
+
+            def copy(engine_copy, piece, column, first, last):
+                engine_copy(
+                    out=places[:, (column + first) // RUN : (column + last) // RUN],
+                    in_=piece[:, :, first:last].rearrange("p t (c i) -> p c t i", i=RUN),
+                )
+
             if i == 0:
-                for s, piece in enumerate((first_piece, second_piece)):
-                    places = grouped[:, s * PIECE : (s + 1) * PIECE].rearrange("p (c i t) -> p c t i", i=RUN, t=PACK)
-                    source = piece.rearrange("p t (c i) -> p c t i", i=RUN)
-                    middle = N_TILE // RUN // 2
-                    nc.scalar.copy(out=places[:, :middle], in_=source[:, :middle])
-                    nc.vector.tensor_copy(out=places[:, middle:], in_=source[:, middle:])
-                grouped_of[i] = grouped
-                return
-            split = first_piece.shape[2]
-            first_places = grouped[:, : split * PACK].rearrange("p (c i t) -> p c t i", i=RUN, t=PACK)
-            second_places = grouped[:, split * PACK :].rearrange("p (c i t) -> p c t i", i=RUN, t=PACK)
-            nc.scalar.copy(out=first_places, in_=first_piece.rearrange("p t (c i) -> p c t i", i=RUN))
-            nc.vector.tensor_copy(out=second_places, in_=second_piece.rearrange("p t (c i) -> p c t i", i=RUN))
+                for s, piece in enumerate(pieces_of[i]):
+                    copy(nc.scalar.copy, piece, s * N_TILE, 0, N_TILE // 2)
+                    copy(nc.vector.tensor_copy, piece, s * N_TILE, N_TILE // 2, N_TILE)
+            elif i < PASSES:
+                first_piece, second_piece = pieces_of[i]
+                copy(nc.scalar.copy, first_piece, 0, 0, SCALAR_COLS_FIRST)
+                copy(nc.vector.tensor_copy, first_piece, 0, SCALAR_COLS_FIRST, N_TILE)
+                copy(nc.vector.tensor_copy, second_piece, N_TILE, 0, N_TILE)
+            else:
+                (piece,) = pieces_of[i]
+                copy(nc.scalar.copy, piece, 0, 0, SCALAR_COLS)
+                copy(nc.vector.tensor_copy, piece, 0, SCALAR_COLS, 2 * N_TILE)
             grouped_of[i] = grouped
 
         def quantise(i):

@@ -20,22 +20,42 @@ PASSES = HIDDEN // K_PASS
 PAIRS = PASSES + HIDDEN // (2 * N_TILE)
 PIECE = PACK * N_TILE
 H_CHUNK = 2
+H_BEHIND = 4
 RUN = 8
 RAW_BUFS = 8
-SCALAR_COLS_FIRST = 384
-SCALAR_COLS = 480
-SEAM = 5
+FINE_PAIRS = 2
 
-BD1_ROWS = HIDDEN // N_TILE
+BD1_ROWS = HIDDEN // P
 BM_ROW = BD1_ROWS
-BV_ROW = BD1_ROWS + 1
-BIAS_ROWS = BD1_ROWS + 2
-SMALL_BEFORE = 5
-FIRST_SPREAD = 8
+BV_ROW = BM_ROW + LATENT // P
+BIAS_ROWS = BV_ROW + LATENT // P
+SPREAD_ROWS = 8
+SMALL_BEFORE = 1
+FIRST_SPREAD = 3
 
+KL_ROUND = 20
 KL_FACTOR = 0.5 / (P * LATENT)
 
 FLOPS = 2 * P * HIDDEN * LATENT * 3
+
+
+TENSOR_COLS = 256
+
+
+def chunks_behind(i):
+    return [c for c in range(PASSES // H_CHUNK) if H_BEHIND + 3 * c // 2 == i]
+
+
+def tensor_columns(i):
+    return TENSOR_COLS if i >= PASSES else 0
+
+
+def scalar_columns(i):
+    if i < FINE_PAIRS:
+        return (224, 224)
+    if i < PASSES:
+        return (512 if i % 2 == 0 else 384, 0)
+    return (640,)
 
 
 def tile_knowledgeawarevariationalautoencoder_pc_k_kernel(
@@ -48,7 +68,7 @@ def tile_knowledgeawarevariationalautoencoder_pc_k_kernel(
         tc.tile_pool(name="h_grouped", bufs=2) as h_grouped_pool,
         tc.tile_pool(name="raw", bufs=RAW_BUFS) as raw_pool,
         tc.tile_pool(name="grouped", bufs=4) as grouped_pool,
-        tc.tile_pool(name="quantised", bufs=SEAM + 2) as quantised_pool,
+        tc.tile_pool(name="quantised", bufs=9) as quantised_pool,
         tc.tile_pool(name="result", bufs=5) as result_pool,
         tc.psum_pool(name="sums", bufs=1) as sums_pool,
         tc.psum_pool(name="banks", bufs=6) as banks,
@@ -67,9 +87,9 @@ def tile_knowledgeawarevariationalautoencoder_pc_k_kernel(
             if i >= PAIRS:
                 return
             if i == SMALL_BEFORE:
-                nc.sync.dma_start(out=bias_rows[0:BD1_ROWS, :], in_=bd1.rearrange("(r n) -> r n", n=N_TILE))
-                nc.sync.dma_start(out=bias_rows[BM_ROW : BM_ROW + 1, :], in_=bm.rearrange("(r n) -> r n", r=1))
-                nc.sync.dma_start(out=bias_rows[BV_ROW : BV_ROW + 1, :], in_=bv.rearrange("(r n) -> r n", r=1))
+                nc.sync.dma_start(out=bias_rows[:BM_ROW, :], in_=bd1.rearrange("(r n) -> r n", n=P))
+                nc.sync.dma_start(out=bias_rows[BM_ROW:BV_ROW, :], in_=bm.rearrange("(r n) -> r n", n=P))
+                nc.sync.dma_start(out=bias_rows[BV_ROW:BIAS_ROWS, :], in_=bv.rearrange("(r n) -> r n", n=P))
                 nc.sync.dma_start(out=eps_sb[:], in_=eps)
             if i < PASSES:
                 raw = raw_pool.tile([P, 2, PIECE], BF16, tag="raw")
@@ -78,8 +98,7 @@ def tile_knowledgeawarevariationalautoencoder_pc_k_kernel(
                 nc.sync.dma_start(out=raw[:, 1, :], in_=Wv[rows, :].rearrange("(p t) n -> p (t n)", t=PACK))
                 by_row = raw[:].rearrange("p s (t n) -> p s t n", t=PACK)
                 pieces_of[i] = (by_row[:, 0], by_row[:, 1])
-                if i % H_CHUNK == H_CHUNK - 1:
-                    chunk = i // H_CHUNK
+                for chunk in chunks_behind(i):
                     h_raw = h_raw_pool.tile([P, H_CHUNK * K_PASS], BF16)
                     nc.sync.dma_start(out=h_raw[:], in_=h[:, chunk * H_CHUNK * K_PASS : (chunk + 1) * H_CHUNK * K_PASS])
                     h_raw_of[chunk] = h_raw
@@ -89,52 +108,81 @@ def tile_knowledgeawarevariationalautoencoder_pc_k_kernel(
                 nc.sync.dma_start(out=raw[:], in_=Wd1[:, cols].rearrange("(p t) n -> p t n", t=PACK))
                 pieces_of[i] = (raw[:],)
 
-        def regroup(i):
-            grouped = grouped_pool.tile([P, 2 * PIECE], BF16, align_bytes=64)
-            places = grouped[:].rearrange("p (c i t) -> p c t i", i=RUN, t=PACK)
+        def views(i, s):
+            piece = pieces_of[i][s]
+            columns = piece.shape[2]
+            source = piece.rearrange("p t (c i) -> p c t i", i=RUN)
+            places = grouped_of[i][:, s * PIECE : s * PIECE + PACK * columns].rearrange(
+                "p (c i t) -> p c t i", i=RUN, t=PACK
+            )
+            return source, places
 
-            def copy(engine_copy, piece, column, first, last):
-                engine_copy(
-                    out=places[:, (column + first) // RUN : (column + last) // RUN],
-                    in_=piece[:, :, first:last].rearrange("p t (c i) -> p c t i", i=RUN),
+        def regroup_left(i, s):
+            if s == 0:
+                grouped = grouped_pool.tile([P, 2 * PIECE], BF16, align_bytes=64)
+                grouped_of[i] = grouped
+            source, places = views(i, s)
+            start = tensor_columns(i) // RUN
+            middle = scalar_columns(i)[s] // RUN
+            if start > 0:
+                turned = banks.tile([P, TENSOR_COLS // P, N_TILE], BF16, tag="bank")
+                for g in range(TENSOR_COLS // P):
+                    nc.tensor.matmul(
+                        turned[:, g, :],
+                        lhsT=ident_bf16[:],
+                        rhs=pieces_of[i][s][:, :, g * P : (g + 1) * P].rearrange("p t c -> p c t"),
+                        start=True,
+                        stop=True,
+                    )
+            if middle > start:
+                nc.scalar.copy(out=places[:, start:middle], in_=source[:, start:middle])
+            if start > 0:
+                nc.scalar.copy(
+                    out=grouped_of[i][:, : TENSOR_COLS * PACK], in_=turned[:].rearrange("p g w -> p (g w)")
                 )
 
-            if i == 0:
-                for s, piece in enumerate(pieces_of[i]):
-                    copy(nc.scalar.copy, piece, s * N_TILE, 0, N_TILE // 2)
-                    copy(nc.vector.tensor_copy, piece, s * N_TILE, N_TILE // 2, N_TILE)
-            elif i < PASSES:
-                first_piece, second_piece = pieces_of[i]
-                copy(nc.scalar.copy, first_piece, 0, 0, SCALAR_COLS_FIRST)
-                copy(nc.vector.tensor_copy, first_piece, 0, SCALAR_COLS_FIRST, N_TILE)
-                copy(nc.vector.tensor_copy, second_piece, N_TILE, 0, N_TILE)
-            else:
-                (piece,) = pieces_of[i]
-                copy(nc.scalar.copy, piece, 0, 0, SCALAR_COLS)
-                copy(nc.vector.tensor_copy, piece, 0, SCALAR_COLS, 2 * N_TILE)
-            grouped_of[i] = grouped
+        def regroup_right(i, s):
+            source, places = views(i, s)
+            middle = scalar_columns(i)[s] // RUN
+            if middle < source.shape[1]:
+                nc.vector.tensor_copy(out=places[:, middle:], in_=source[:, middle:])
 
-        def quantise(i):
-            words = quantised_pool.tile([P, 2 * N_TILE], U32, align_bytes=64)
-            scales = quantised_pool.tile([P, 2 * N_TILE], U8, align_bytes=64)
-            nc.vector.quantize_mx(out=words[:].bitcast(FP8X4), scales=scales[:], in_=grouped_of[i][:])
-            words_of[i] = words
-            scales_of[i] = scales
+        def quantise(i, first, last):
+            if first == 0:
+                words = quantised_pool.tile([P, 2 * N_TILE], U32, align_bytes=64)
+                scales = quantised_pool.tile([P, 2 * N_TILE], U8, align_bytes=64)
+                words_of[i] = words
+                scales_of[i] = scales
+            nc.vector.quantize_mx(
+                out=words_of[i][:, first:last].bitcast(FP8X4),
+                scales=scales_of[i][:, first:last],
+                in_=grouped_of[i][:, PACK * first : PACK * last],
+            )
 
-        def prepare(i):
-            if i < PAIRS:
-                regroup(i)
-                load(i + RAW_BUFS)
-            if i >= 1:
-                quantise(i - 1)
+        def start_pair(i):
+            for s in range(len(pieces_of[i])):
+                regroup_left(i, s)
+                regroup_right(i, s)
+                if i < FINE_PAIRS:
+                    if s == 1:
+                        quantise(i, 0, N_TILE)
+                    elif i > 0:
+                        quantise(i - 1, N_TILE, 2 * N_TILE)
+            load(i + RAW_BUFS)
 
-        def multiply(out, stationary_words, stationary_scales, i, j, start, stop):
+        def finish_pair(i):
+            if i >= FINE_PAIRS:
+                quantise(i, 0, 2 * N_TILE)
+            elif i == FINE_PAIRS - 1:
+                quantise(i, N_TILE, 2 * N_TILE)
+
+        def multiply(out, stationary_words, stationary_scales, i, first, last, start, stop):
             nc.tensor.matmul_mx(
                 out=out,
                 lhsT=stationary_words.bitcast(FP8X4),
                 lhsT_scale=stationary_scales,
-                rhs=words_of[i][:, j * N_TILE : (j + 1) * N_TILE].bitcast(FP8X4),
-                rhs_scale=scales_of[i][:, j * N_TILE : (j + 1) * N_TILE],
+                rhs=words_of[i][:, first:last].bitcast(FP8X4),
+                rhs_scale=scales_of[i][:, first:last],
                 start=start,
                 stop=stop,
             )
@@ -149,7 +197,7 @@ def tile_knowledgeawarevariationalautoencoder_pc_k_kernel(
         plus_factor = keep.tile([P, P], F32)
         nc.gpsimd.memset(plus_factor[:], KL_FACTOR)
 
-        bias_rows = keep.tile([P, N_TILE], BF16)
+        bias_rows = keep.tile([P, P], BF16)
         nc.vector.memset(bias_rows[:].bitcast(I32), 0)
         eps_sb = keep.tile([P, LATENT], BF16)
 
@@ -179,19 +227,23 @@ def tile_knowledgeawarevariationalautoencoder_pc_k_kernel(
                 in_=h_grouped_of[chunk][:],
             )
 
-        bias_all = keep.tile([P, BIAS_ROWS, N_TILE], BF16)
+        bias_cols = keep.tile([P, P], BF16)
+        bias_all = keep.tile([P, BIAS_ROWS * P], BF16)
 
-        def spread_bias(r):
-            spread = banks.tile([P, 2, N_TILE], BF16, tag="bank")
-            for j in range(2):
-                nc.tensor.matmul(
-                    spread[:, j, :],
-                    lhsT=ident_bf16[:, r + j : r + j + 1].to_broadcast([P, P]),
-                    rhs=bias_rows[:],
-                    start=True,
-                    stop=True,
+        def turn_biases():
+            turned = banks.tile([P, P], BF16, tag="bank")
+            nc.tensor.transpose(turned[:], bias_rows[:], ident_bf16[:])
+            nc.scalar.copy(out=bias_cols[:], in_=turned[:])
+
+        def spread_biases(r):
+            spread = banks.tile([P, SPREAD_ROWS, P], BF16, tag="bank")
+            for j in range(SPREAD_ROWS):
+                nc.tensor.transpose(
+                    spread[:, j, :], bias_cols[:, r + j : r + j + 1].to_broadcast([P, P]), ident_bf16[:]
                 )
-            nc.scalar.copy(out=bias_all[:, r : r + 2, :], in_=spread[:])
+            nc.scalar.copy(
+                out=bias_all[:, r * P : (r + SPREAD_ROWS) * P], in_=spread[:].rearrange("p j n -> p (j n)")
+            )
 
         mean_sum = sums_pool.tile([P, LATENT], F32)
         var_sum = sums_pool.tile([P, LATENT], F32)
@@ -203,52 +255,64 @@ def tile_knowledgeawarevariationalautoencoder_pc_k_kernel(
                     h_words[:, c * P : (c + 1) * P],
                     h_scales[:, c * P : (c + 1) * P],
                     c,
-                    j,
+                    j * N_TILE,
+                    (j + 1) * N_TILE,
                     start=(c == 0),
                     stop=(c == PASSES - 1),
                 )
 
-        for i in range(PASSES + 2):
-            prepare(i)
-            if i < PASSES and i % H_CHUNK == H_CHUNK - 1:
-                turn_h(i // H_CHUNK)
-            if 1 <= i <= PASSES and (i - 1) % H_CHUNK == H_CHUNK - 1:
-                quantise_h((i - 1) // H_CHUNK)
-            if i % H_CHUNK == H_CHUNK - 1 and i > H_CHUNK:
-                for c in range(i - 1 - H_CHUNK, i - 1):
+        multiplied = 0
+        quantised_before = []
+        for i in range(PASSES):
+            start_pair(i)
+            if i > 0:
+                finish_pair(i - 1)
+            for chunk in chunks_behind(i):
+                turn_h(chunk)
+            for chunk in chunks_behind(i - 1):
+                quantise_h(chunk)
+            while multiplied < PASSES and multiplied + H_CHUNK < i and multiplied // H_CHUNK in quantised_before:
+                for c in range(multiplied, multiplied + H_CHUNK):
                     multiply_first(c)
-            r = 2 * (i - FIRST_SPREAD)
+                multiplied += H_CHUNK
+            quantised_before.extend(chunks_behind(i - 1))
+            if i == FIRST_SPREAD - 1:
+                turn_biases()
+            r = SPREAD_ROWS * (i - FIRST_SPREAD)
             if 0 <= r < BIAS_ROWS:
-                spread_bias(r)
+                spread_biases(r)
+
+        regroup_left(PASSES, 0)
+        finish_pair(PASSES - 1)
+        for c in range(multiplied, PASSES):
+            multiply_first(c)
+        regroup_right(PASSES, 0)
+        load(PASSES + RAW_BUFS)
 
 
         z_mean = keep.tile([P, LATENT], F32)
-        nc.vector.tensor_tensor(out=z_mean[:], in0=mean_sum[:], in1=bias_all[:, BM_ROW, :], op=ALU.add)
+        nc.vector.tensor_tensor(out=z_mean[:], in0=mean_sum[:], in1=bias_all[:, BM_ROW * P : BV_ROW * P], op=ALU.add)
         z_log_var = keep.tile([P, LATENT], F32)
         sum_log_var = keep.tile([P, 1], F32)
         nc.vector.scalar_tensor_tensor(
             out=z_log_var[:],
             in0=var_sum[:],
             scalar=1.0,
-            in1=bias_all[:, BV_ROW, :],
+            in1=bias_all[:, BV_ROW * P : BIAS_ROWS * P],
             op0=ALU.mult,
             op1=ALU.add,
             accum_out=sum_log_var[:],
         )
 
-        prepare(PASSES + 2)
-
+        regroup_left(PASSES + 1, 0)
         sigma = keep.tile([P, LATENT], F32)
         nc.scalar.activation(out=sigma[:], in_=z_log_var[:], func=ACT.Exp, scale=0.5)
-        squares = keep.tile([P, LATENT], F32)
-        sum_squares = keep.tile([P, 1], F32)
-        nc.scalar.activation(out=squares[:], in_=z_mean[:], func=ACT.Square, accum_out=sum_squares[:])
-        variances = keep.tile([P, LATENT], F32)
-        sum_variances = keep.tile([P, 1], F32)
-        nc.scalar.activation(out=variances[:], in_=z_log_var[:], func=ACT.Exp, accum_out=sum_variances[:])
-
+        finish_pair(PASSES)
         noise = keep.tile([P, LATENT], F32)
         nc.vector.tensor_tensor(out=noise[:], in0=sigma[:], in1=eps_sb[:], op=ALU.mult)
+        regroup_right(PASSES + 1, 0)
+        load(PASSES + 1 + RAW_BUFS)
+        regroup_left(PASSES + 2, 0)
         z_sorted = keep.tile([P, PACK, P], BF16)
         nc.vector.tensor_tensor(
             out=z_sorted[:],
@@ -259,55 +323,78 @@ def tile_knowledgeawarevariationalautoencoder_pc_k_kernel(
         z_turned = banks.tile([P, PACK, P], BF16, tag="bank")
         for t in range(PACK):
             nc.tensor.transpose(z_turned[:, t, :], z_sorted[:, t, :], ident_bf16[:])
-
-        prepare(PASSES + 3)
-
+        finish_pair(PASSES + 1)
         z_grouped = keep.tile([P, P * PACK], BF16, align_bytes=64)
         nc.vector.tensor_copy(
             out=z_grouped[:].rearrange("p (b t) -> p b t", t=PACK),
             in_=z_turned[:].rearrange("p t b -> p b t"),
         )
-        kl_sum = banks.tile([P, 1], F32, tag="bank")
-        for n, (factor, row_sums) in enumerate(
-            ((minus_factor, sum_log_var), (plus_factor, sum_squares), (plus_factor, sum_variances))
-        ):
-            nc.tensor.matmul(kl_sum[:], lhsT=factor[:], rhs=row_sums[:], start=(n == 0), stop=(n == 2))
-
-        prepare(PASSES + 4)
-
+        regroup_right(PASSES + 2, 0)
+        load(PASSES + 2 + RAW_BUFS)
         z_words = keep.tile([P, P], U32, align_bytes=64)
         z_scales = keep.tile([P, P], U8, align_bytes=64)
         nc.vector.quantize_mx(out=z_words[:].bitcast(FP8X4), scales=z_scales[:], in_=z_grouped[:])
-        kl = keep.tile([P, 1], F32)
-        nc.vector.tensor_scalar_add(out=kl[:], in0=kl_sum[:], scalar1=-0.5)
-        nc.sync.dma_start(out=out_1.rearrange("(a b) -> a b", a=1), in_=kl[0:1, 0:1])
 
 
-        def project(i):
-            result = result_pool.tile([P, 2, N_TILE], F32)
-            for j in range(2):
-                product = banks.tile([P, N_TILE], F32, tag="bank")
-                multiply(product[:], z_words[:], z_scales[:], i, j, start=True, stop=True)
-                nc.vector.tensor_tensor(
-                    out=result[:, j, :], in0=product[:], in1=bias_all[:, 2 * (i - PASSES) + j, :], op=ALU.add
-                )
-            result_of[i] = result
+        sum_squares = keep.tile([P, 1], F32)
+        sum_variances = keep.tile([P, 1], F32)
 
-        def squash(i):
-            result = result_of[i]
-            nc.scalar.activation(out=result[:], in_=result[:], func=ACT.Tanh)
-            cols = slice((i - PASSES) * 2 * N_TILE, (i - PASSES + 1) * 2 * N_TILE)
-            nc.scalar.dma_start(out=out_0[:, cols], in_=result[:].rearrange("b j n -> b (j n)"))
+        def sum_rows_for_kl():
+            unread = keep.tile([P, LATENT], F32)
+            nc.scalar.activation(out=unread[:], in_=z_mean[:], func=ACT.Square, accum_out=sum_squares[:])
+            nc.scalar.activation(out=unread[:], in_=z_log_var[:], func=ACT.Exp, accum_out=sum_variances[:])
 
-        projected = PASSES
-        squashed = PASSES
-        for i in range(PASSES + SEAM, PAIRS + 3):
-            if i <= PAIRS:
-                prepare(i)
-            ready = projected
-            for j in range(projected, min(projected + 2, i - 1, PAIRS)):
-                project(j)
-                projected = j + 1
-            for j in range(squashed, ready):
-                squash(j)
-                squashed = j + 1
+        def finish_kl():
+            kl_sum = banks.tile([P, 1], F32, tag="bank")
+            for n, (factor, row_sums) in enumerate(
+                ((minus_factor, sum_log_var), (plus_factor, sum_squares), (plus_factor, sum_variances))
+            ):
+                nc.tensor.matmul(kl_sum[:], lhsT=factor[:], rhs=row_sums[:], start=(n == 0), stop=(n == 2))
+
+            kl = keep.tile([P, 1], F32)
+            nc.vector.tensor_scalar_add(out=kl[:], in0=kl_sum[:], scalar1=-0.5)
+            nc.sync.dma_start(out=out_1.rearrange("(a b) -> a b", a=1), in_=kl[0:1, 0:1])
+
+
+        def project(i, first, last):
+            if first == 0:
+                result = result_pool.tile([P, 2 * N_TILE], F32)
+                result_of[i] = result
+            product = banks.tile([P, N_TILE], F32, tag="bank")
+            width = last - first
+            multiply(product[:, :width], z_words[:], z_scales[:], i, first, last, start=True, stop=True)
+            column = (i - PASSES) * 2 * N_TILE + first
+            nc.vector.tensor_tensor(
+                out=result_of[i][:, first:last],
+                in0=product[:, :width],
+                in1=bias_all[:, column : column + width],
+                op=ALU.add,
+            )
+
+        def squash(i, first, last):
+            part = result_of[i][:, first:last]
+            nc.scalar.activation(out=part, in_=part, func=ACT.Tanh)
+            column = (i - PASSES) * 2 * N_TILE
+            nc.sync.dma_start(out=out_0[:, column + first : column + last], in_=part)
+
+        for i in range(PASSES + 3, PAIRS + 1):
+            if i < PAIRS:
+                start_pair(i)
+            finish_pair(i - 1)
+            for j in (PASSES, PASSES + 1) if i == PASSES + 3 else (i - 2,):
+                project(j, 0, N_TILE)
+                project(j, N_TILE, 2 * N_TILE)
+            if i > PASSES + 3:
+                squash(i - 3, 0, 2 * N_TILE)
+            if i == PASSES + 4:
+                squash(PASSES, 0, 2 * N_TILE)
+            if i == KL_ROUND:
+                sum_rows_for_kl()
+            if i == KL_ROUND + 1:
+                finish_kl()
+
+        last = PAIRS - 1
+        squash(last - 1, 0, 2 * N_TILE)
+        for first, after in ((0, N_TILE), (N_TILE, 3 * N_TILE // 2), (3 * N_TILE // 2, 2 * N_TILE)):
+            project(last, first, after)
+            squash(last, first, after)

@@ -20,7 +20,7 @@ PASSES = HIDDEN // K_PASS
 PAIRS = PASSES + HIDDEN // (2 * N_TILE)
 PIECE = PACK * N_TILE
 H_CHUNK = 2
-H_BEHIND = 4
+H_BEHIND = 3
 RUN = 8
 RAW_BUFS = 8
 FINE_PAIRS = 2
@@ -30,7 +30,8 @@ BM_ROW = BD1_ROWS
 BV_ROW = BM_ROW + LATENT // P
 BIAS_ROWS = BV_ROW + LATENT // P
 SPREAD_ROWS = 8
-SMALL_BEFORE = 1
+BIASES_BEFORE = 1
+EPS_BEFORE = 12
 FIRST_SPREAD = 3
 
 KL_ROUND = 20
@@ -54,8 +55,8 @@ def scalar_columns(i):
     if i < FINE_PAIRS:
         return (224, 224)
     if i < PASSES:
-        return (512 if i % 2 == 0 else 384, 0)
-    return (640,)
+        return (448 if i % 2 == 0 else 384, 0)
+    return (608,)
 
 
 def tile_knowledgeawarevariationalautoencoder_pc_k_kernel(
@@ -86,10 +87,11 @@ def tile_knowledgeawarevariationalautoencoder_pc_k_kernel(
         def load(i):
             if i >= PAIRS:
                 return
-            if i == SMALL_BEFORE:
+            if i == BIASES_BEFORE:
                 nc.sync.dma_start(out=bias_rows[:BM_ROW, :], in_=bd1.rearrange("(r n) -> r n", n=P))
                 nc.sync.dma_start(out=bias_rows[BM_ROW:BV_ROW, :], in_=bm.rearrange("(r n) -> r n", n=P))
                 nc.sync.dma_start(out=bias_rows[BV_ROW:BIAS_ROWS, :], in_=bv.rearrange("(r n) -> r n", n=P))
+            if i == EPS_BEFORE:
                 nc.sync.dma_start(out=eps_sb[:], in_=eps)
             if i < PASSES:
                 raw = raw_pool.tile([P, 2, PIECE], BF16, tag="raw")
@@ -380,14 +382,13 @@ def tile_knowledgeawarevariationalautoencoder_pc_k_kernel(
         for i in range(PASSES + 3, PAIRS + 1):
             if i < PAIRS:
                 start_pair(i)
+            if i == PASSES + 3:
+                project(PASSES, 0, N_TILE)
+                project(PASSES, N_TILE, 2 * N_TILE)
             finish_pair(i - 1)
-            for j in (PASSES, PASSES + 1) if i == PASSES + 3 else (i - 2,):
-                project(j, 0, N_TILE)
-                project(j, N_TILE, 2 * N_TILE)
-            if i > PASSES + 3:
-                squash(i - 3, 0, 2 * N_TILE)
-            if i == PASSES + 4:
-                squash(PASSES, 0, 2 * N_TILE)
+            project(i - 2, 0, N_TILE)
+            project(i - 2, N_TILE, 2 * N_TILE)
+            squash(i - 3, 0, 2 * N_TILE)
             if i == KL_ROUND:
                 sum_rows_for_kl()
             if i == KL_ROUND + 1:

import concourse.mybir as mybir
from concourse.masks import make_identity

F32 = mybir.dt.float32
BF16 = mybir.dt.bfloat16
I32 = mybir.dt.int32
U32 = mybir.dt.uint32
U8 = mybir.dt.uint8
FP8X4 = mybir.dt.float8_e4m3fn_x4
ACT = mybir.ActivationFunctionType
ALU = mybir.AluOpType

P = 128
PACK = 4
K_PASS = P * PACK
N_TILE = 512
HIDDEN = 8192
LATENT = 512
PASSES = HIDDEN // K_PASS
PAIRS = PASSES + HIDDEN // (2 * N_TILE)
PIECE = PACK * N_TILE
H_CHUNK = 2
H_BEHIND = 3
RUN = 8
RAW_BUFS = 8
FINE_PAIRS = 2

BD1_ROWS = HIDDEN // P
BM_ROW = BD1_ROWS
BV_ROW = BM_ROW + LATENT // P
BIAS_ROWS = BV_ROW + LATENT // P
SPREAD_ROWS = 8
BIASES_BEFORE = 1
EPS_BEFORE = 12
FIRST_SPREAD = 3

KL_ROUND = 20
KL_FACTOR = 0.5 / (P * LATENT)

FLOPS = 2 * P * HIDDEN * LATENT * 3


TENSOR_COLS = 256


def chunks_behind(i):
    return [c for c in range(PASSES // H_CHUNK) if H_BEHIND + 3 * c // 2 == i]


def tensor_columns(i):
    return TENSOR_COLS if i >= PASSES else 0


def scalar_columns(i):
    if i < FINE_PAIRS:
        return (224, 224)
    if i < PASSES:
        return (448 if i % 2 == 0 else 384, 0)
    return (608,)


def tile_knowledgeawarevariationalautoencoder_pc_k_kernel(
    tc, h, Wm, bm, Wv, bv, eps, Wd1, bd1, out_0, out_1
):
    nc = tc.nc
    with (
        tc.tile_pool(name="keep", bufs=1) as keep,
        tc.tile_pool(name="h_raw", bufs=PASSES // H_CHUNK) as h_raw_pool,
        tc.tile_pool(name="h_grouped", bufs=2) as h_grouped_pool,
        tc.tile_pool(name="raw", bufs=RAW_BUFS) as raw_pool,
        tc.tile_pool(name="grouped", bufs=4) as grouped_pool,
        tc.tile_pool(name="quantised", bufs=9) as quantised_pool,
        tc.tile_pool(name="result", bufs=5) as result_pool,
        tc.psum_pool(name="sums", bufs=1) as sums_pool,
        tc.psum_pool(name="banks", bufs=6) as banks,
        tc.manual_schedule(),
    ):
        h_raw_of = {}
        h_grouped_of = {}
        pieces_of = {}
        grouped_of = {}
        words_of = {}
        scales_of = {}
        result_of = {}


        def load(i):
            if i >= PAIRS:
                return
            if i == BIASES_BEFORE:
                nc.sync.dma_start(out=bias_rows[:BM_ROW, :], in_=bd1.rearrange("(r n) -> r n", n=P))
                nc.sync.dma_start(out=bias_rows[BM_ROW:BV_ROW, :], in_=bm.rearrange("(r n) -> r n", n=P))
                nc.sync.dma_start(out=bias_rows[BV_ROW:BIAS_ROWS, :], in_=bv.rearrange("(r n) -> r n", n=P))
            if i == EPS_BEFORE:
                nc.sync.dma_start(out=eps_sb[:], in_=eps)
            if i < PASSES:
                raw = raw_pool.tile([P, 2, PIECE], BF16, tag="raw")
                rows = slice(i * K_PASS, (i + 1) * K_PASS)
                nc.sync.dma_start(out=raw[:, 0, :], in_=Wm[rows, :].rearrange("(p t) n -> p (t n)", t=PACK))
                nc.sync.dma_start(out=raw[:, 1, :], in_=Wv[rows, :].rearrange("(p t) n -> p (t n)", t=PACK))
                by_row = raw[:].rearrange("p s (t n) -> p s t n", t=PACK)
                pieces_of[i] = (by_row[:, 0], by_row[:, 1])
                for chunk in chunks_behind(i):
                    h_raw = h_raw_pool.tile([P, H_CHUNK * K_PASS], BF16)
                    nc.sync.dma_start(out=h_raw[:], in_=h[:, chunk * H_CHUNK * K_PASS : (chunk + 1) * H_CHUNK * K_PASS])
                    h_raw_of[chunk] = h_raw
            else:
                raw = raw_pool.tile([P, PACK, 2 * N_TILE], BF16, tag="raw")
                cols = slice((i - PASSES) * 2 * N_TILE, (i - PASSES + 1) * 2 * N_TILE)
                nc.sync.dma_start(out=raw[:], in_=Wd1[:, cols].rearrange("(p t) n -> p t n", t=PACK))
                pieces_of[i] = (raw[:],)

        def views(i, s):
            piece = pieces_of[i][s]
            columns = piece.shape[2]
            source = piece.rearrange("p t (c i) -> p c t i", i=RUN)
            places = grouped_of[i][:, s * PIECE : s * PIECE + PACK * columns].rearrange(
                "p (c i t) -> p c t i", i=RUN, t=PACK
            )
            return source, places

        def regroup_left(i, s):
            if s == 0:
                grouped = grouped_pool.tile([P, 2 * PIECE], BF16, align_bytes=64)
                grouped_of[i] = grouped
            source, places = views(i, s)
            start = tensor_columns(i) // RUN
            middle = scalar_columns(i)[s] // RUN
            if start > 0:
                turned = banks.tile([P, TENSOR_COLS // P, N_TILE], BF16, tag="bank")
                for g in range(TENSOR_COLS // P):
                    nc.tensor.matmul(
                        turned[:, g, :],
                        lhsT=ident_bf16[:],
                        rhs=pieces_of[i][s][:, :, g * P : (g + 1) * P].rearrange("p t c -> p c t"),
                        start=True,
                        stop=True,
                    )
            if middle > start:
                nc.scalar.copy(out=places[:, start:middle], in_=source[:, start:middle])
            if start > 0:
                nc.scalar.copy(
                    out=grouped_of[i][:, : TENSOR_COLS * PACK], in_=turned[:].rearrange("p g w -> p (g w)")
                )

        def regroup_right(i, s):
            source, places = views(i, s)
            middle = scalar_columns(i)[s] // RUN
            if middle < source.shape[1]:
                nc.vector.tensor_copy(out=places[:, middle:], in_=source[:, middle:])

        def quantise(i, first, last):
            if first == 0:
                words = quantised_pool.tile([P, 2 * N_TILE], U32, align_bytes=64)
                scales = quantised_pool.tile([P, 2 * N_TILE], U8, align_bytes=64)
                words_of[i] = words
                scales_of[i] = scales
            nc.vector.quantize_mx(
                out=words_of[i][:, first:last].bitcast(FP8X4),
                scales=scales_of[i][:, first:last],
                in_=grouped_of[i][:, PACK * first : PACK * last],
            )

        def start_pair(i):
            for s in range(len(pieces_of[i])):
                regroup_left(i, s)
                regroup_right(i, s)
                if i < FINE_PAIRS:
                    if s == 1:
                        quantise(i, 0, N_TILE)
                    elif i > 0:
                        quantise(i - 1, N_TILE, 2 * N_TILE)
            load(i + RAW_BUFS)

        def finish_pair(i):
            if i >= FINE_PAIRS:
                quantise(i, 0, 2 * N_TILE)
            elif i == FINE_PAIRS - 1:
                quantise(i, N_TILE, 2 * N_TILE)

        def multiply(out, stationary_words, stationary_scales, i, first, last, start, stop):
            nc.tensor.matmul_mx(
                out=out,
                lhsT=stationary_words.bitcast(FP8X4),
                lhsT_scale=stationary_scales,
                rhs=words_of[i][:, first:last].bitcast(FP8X4),
                rhs_scale=scales_of[i][:, first:last],
                start=start,
                stop=stop,
            )


        ident_f32 = keep.tile([P, P], F32)
        make_identity(nc, ident_f32[:])
        ident_bf16 = keep.tile([P, P], BF16)
        make_identity(nc, ident_bf16[:])
        minus_factor = keep.tile([P, P], F32)
        nc.gpsimd.memset(minus_factor[:], -KL_FACTOR)
        plus_factor = keep.tile([P, P], F32)
        nc.gpsimd.memset(plus_factor[:], KL_FACTOR)

        bias_rows = keep.tile([P, P], BF16)
        nc.vector.memset(bias_rows[:].bitcast(I32), 0)
        eps_sb = keep.tile([P, LATENT], BF16)

        for i in range(RAW_BUFS):
            load(i)


        h_words = keep.tile([P, PASSES * P], U32, align_bytes=64)
        h_scales = keep.tile([P, PASSES * P], U8, align_bytes=64)

        def turn_h(chunk):
            pairs = h_raw_of[chunk][:].bitcast(F32).rearrange("b (g p u) -> b g u p", g=H_CHUNK, u=2)
            h_grouped = h_grouped_pool.tile([P, H_CHUNK * K_PASS], BF16, align_bytes=64)
            h_places = h_grouped[:].bitcast(F32).rearrange("p (g b u) -> p g b u", g=H_CHUNK, u=2)
            turned = banks.tile([P, H_CHUNK, 2, P], F32, tag="bank")
            for g in range(H_CHUNK):
                for u in range(2):
                    nc.tensor.transpose(turned[:, g, u, :], pairs[:, g, u, :], ident_f32[:])
            nc.scalar.copy(out=h_places, in_=turned[:].rearrange("p g u b -> p g b u"))
            h_grouped_of[chunk] = h_grouped

        def quantise_h(chunk):
            chunk_cols = slice(chunk * H_CHUNK * P, (chunk + 1) * H_CHUNK * P)
            nc.vector.quantize_mx(
                out=h_words[:, chunk_cols].bitcast(FP8X4),
                scales=h_scales[:, chunk_cols],
                in_=h_grouped_of[chunk][:],
            )

        bias_cols = keep.tile([P, P], BF16)
        bias_all = keep.tile([P, BIAS_ROWS * P], BF16)

        def turn_biases():
            turned = banks.tile([P, P], BF16, tag="bank")
            nc.tensor.transpose(turned[:], bias_rows[:], ident_bf16[:])
            nc.scalar.copy(out=bias_cols[:], in_=turned[:])

        def spread_biases(r):
            spread = banks.tile([P, SPREAD_ROWS, P], BF16, tag="bank")
            for j in range(SPREAD_ROWS):
                nc.tensor.transpose(
                    spread[:, j, :], bias_cols[:, r + j : r + j + 1].to_broadcast([P, P]), ident_bf16[:]
                )
            nc.scalar.copy(
                out=bias_all[:, r * P : (r + SPREAD_ROWS) * P], in_=spread[:].rearrange("p j n -> p (j n)")
            )

        mean_sum = sums_pool.tile([P, LATENT], F32)
        var_sum = sums_pool.tile([P, LATENT], F32)

        def multiply_first(c):
            for j, running_sum in enumerate((mean_sum, var_sum)):
                multiply(
                    running_sum[:],
                    h_words[:, c * P : (c + 1) * P],
                    h_scales[:, c * P : (c + 1) * P],
                    c,
                    j * N_TILE,
                    (j + 1) * N_TILE,
                    start=(c == 0),
                    stop=(c == PASSES - 1),
                )

        multiplied = 0
        quantised_before = []
        for i in range(PASSES):
            start_pair(i)
            if i > 0:
                finish_pair(i - 1)
            for chunk in chunks_behind(i):
                turn_h(chunk)
            for chunk in chunks_behind(i - 1):
                quantise_h(chunk)
            while multiplied < PASSES and multiplied + H_CHUNK < i and multiplied // H_CHUNK in quantised_before:
                for c in range(multiplied, multiplied + H_CHUNK):
                    multiply_first(c)
                multiplied += H_CHUNK
            quantised_before.extend(chunks_behind(i - 1))
            if i == FIRST_SPREAD - 1:
                turn_biases()
            r = SPREAD_ROWS * (i - FIRST_SPREAD)
            if 0 <= r < BIAS_ROWS:
                spread_biases(r)

        regroup_left(PASSES, 0)
        finish_pair(PASSES - 1)
        for c in range(multiplied, PASSES):
            multiply_first(c)
        regroup_right(PASSES, 0)
        load(PASSES + RAW_BUFS)


        z_mean = keep.tile([P, LATENT], F32)
        nc.vector.tensor_tensor(out=z_mean[:], in0=mean_sum[:], in1=bias_all[:, BM_ROW * P : BV_ROW * P], op=ALU.add)
        z_log_var = keep.tile([P, LATENT], F32)
        sum_log_var = keep.tile([P, 1], F32)
        nc.vector.scalar_tensor_tensor(
            out=z_log_var[:],
            in0=var_sum[:],
            scalar=1.0,
            in1=bias_all[:, BV_ROW * P : BIAS_ROWS * P],
            op0=ALU.mult,
            op1=ALU.add,
            accum_out=sum_log_var[:],
        )

        regroup_left(PASSES + 1, 0)
        sigma = keep.tile([P, LATENT], F32)
        nc.scalar.activation(out=sigma[:], in_=z_log_var[:], func=ACT.Exp, scale=0.5)
        finish_pair(PASSES)
        noise = keep.tile([P, LATENT], F32)
        nc.vector.tensor_tensor(out=noise[:], in0=sigma[:], in1=eps_sb[:], op=ALU.mult)
        regroup_right(PASSES + 1, 0)
        load(PASSES + 1 + RAW_BUFS)
        regroup_left(PASSES + 2, 0)
        z_sorted = keep.tile([P, PACK, P], BF16)
        nc.vector.tensor_tensor(
            out=z_sorted[:],
            in0=z_mean[:].rearrange("b (p t) -> b t p", t=PACK),
            in1=noise[:].rearrange("b (p t) -> b t p", t=PACK),
            op=ALU.add,
        )
        z_turned = banks.tile([P, PACK, P], BF16, tag="bank")
        for t in range(PACK):
            nc.tensor.transpose(z_turned[:, t, :], z_sorted[:, t, :], ident_bf16[:])
        finish_pair(PASSES + 1)
        z_grouped = keep.tile([P, P * PACK], BF16, align_bytes=64)
        nc.vector.tensor_copy(
            out=z_grouped[:].rearrange("p (b t) -> p b t", t=PACK),
            in_=z_turned[:].rearrange("p t b -> p b t"),
        )
        regroup_right(PASSES + 2, 0)
        load(PASSES + 2 + RAW_BUFS)
        z_words = keep.tile([P, P], U32, align_bytes=64)
        z_scales = keep.tile([P, P], U8, align_bytes=64)
        nc.vector.quantize_mx(out=z_words[:].bitcast(FP8X4), scales=z_scales[:], in_=z_grouped[:])


        sum_squares = keep.tile([P, 1], F32)
        sum_variances = keep.tile([P, 1], F32)

        def sum_rows_for_kl():
            unread = keep.tile([P, LATENT], F32)
            nc.scalar.activation(out=unread[:], in_=z_mean[:], func=ACT.Square, accum_out=sum_squares[:])
            nc.scalar.activation(out=unread[:], in_=z_log_var[:], func=ACT.Exp, accum_out=sum_variances[:])

        def finish_kl():
            kl_sum = banks.tile([P, 1], F32, tag="bank")
            for n, (factor, row_sums) in enumerate(
                ((minus_factor, sum_log_var), (plus_factor, sum_squares), (plus_factor, sum_variances))
            ):
                nc.tensor.matmul(kl_sum[:], lhsT=factor[:], rhs=row_sums[:], start=(n == 0), stop=(n == 2))

            kl = keep.tile([P, 1], F32)
            nc.vector.tensor_scalar_add(out=kl[:], in0=kl_sum[:], scalar1=-0.5)
            nc.sync.dma_start(out=out_1.rearrange("(a b) -> a b", a=1), in_=kl[0:1, 0:1])


        def project(i, first, last):
            if first == 0:
                result = result_pool.tile([P, 2 * N_TILE], F32)
                result_of[i] = result
            product = banks.tile([P, N_TILE], F32, tag="bank")
            width = last - first
            multiply(product[:, :width], z_words[:], z_scales[:], i, first, last, start=True, stop=True)
            column = (i - PASSES) * 2 * N_TILE + first
            nc.vector.tensor_tensor(
                out=result_of[i][:, first:last],
                in0=product[:, :width],
                in1=bias_all[:, column : column + width],
                op=ALU.add,
            )

        def squash(i, first, last):
            part = result_of[i][:, first:last]
            nc.scalar.activation(out=part, in_=part, func=ACT.Tanh)
            column = (i - PASSES) * 2 * N_TILE
            nc.sync.dma_start(out=out_0[:, column + first : column + last], in_=part)

        for i in range(PASSES + 3, PAIRS + 1):
            if i < PAIRS:
                start_pair(i)
            if i == PASSES + 3:
                project(PASSES, 0, N_TILE)
                project(PASSES, N_TILE, 2 * N_TILE)
            finish_pair(i - 1)
            project(i - 2, 0, N_TILE)
            project(i - 2, N_TILE, 2 * N_TILE)
            squash(i - 3, 0, 2 * N_TILE)
            if i == KL_ROUND:
                sum_rows_for_kl()
            if i == KL_ROUND + 1:
                finish_kl()

        last = PAIRS - 1
        squash(last - 1, 0, 2 * N_TILE)
        for first, after in ((0, N_TILE), (N_TILE, 3 * N_TILE // 2), (3 * N_TILE // 2, 2 * N_TILE)):
            project(last, first, after)
            squash(last, first, after)
